import numpy as np
import ml_dtypes


def mxq(x, axis, fmt="e4m3"):
    dtype, down = {"e4m3": (ml_dtypes.float8_e4m3fn, 7), "e5m2": (ml_dtypes.float8_e5m2, 14)}[fmt]
    v = np.moveaxis(np.asarray(x, np.float32).astype(ml_dtypes.bfloat16).astype(np.float64), axis, -1)
    blocks = v.reshape(v.shape[:-1] + (-1, 32))
    amax = np.abs(blocks).max(-1, keepdims=True)
    byte = np.maximum(np.where(amax > 0, np.frexp(amax)[1] - 1 + 127, 0) - down, 1)
    scale = np.exp2(byte - 127.0)
    codes = (blocks / scale).astype(np.float32).astype(dtype).astype(np.float64)
    return np.moveaxis((codes * scale).reshape(v.shape), -1, axis)


WIDE = False


def mx_kscale(k):
    if not WIDE:
        return np.ones(k)
    levels = np.array([10, -10, 5, -5, 0])
    if k % 512:
        return np.exp2(np.random.permutation(np.resize(levels, k // 32))).repeat(32)
    a = np.empty((k // 512, 16))
    for p in range(k // 512):
        a[p, :8] = np.random.permutation(np.resize(levels, 8))
        for g in range(8):
            far = levels[np.abs(levels - a[p, g]) >= 10]
            a[p, g + 8] = far[np.random.randint(len(far))]
    return np.exp2(a.ravel()).repeat(32)


BF16 = ml_dtypes.bfloat16


def bf(x):
    return np.asarray(x, np.float32).astype(BF16)


def f64(x):
    return np.asarray(x).astype(np.float64)


N, F, M, E, H, G, C = 2048, 1024, 512, 512, 256, 128, 10


def draw_adj():
    p = np.random.standard_normal(N)
    return np.exp(1.5 * np.random.standard_normal((N, N)) + 0.5 * p[:, None] + 0.5 * p[None, :]) * 0.3 / N


def draw0():
    u, s = mx_kscale(E), mx_kscale(N)
    c = s / np.exp2(np.round(np.log2(s.mean())))
    return {"h_enc": bf(np.maximum(np.random.standard_normal((N, E)), 0.0) * u / c[:, None]),
            "adj": bf(draw_adj() * c),
            "gcn1_w": bf(np.random.standard_normal((E, H)) * 1.5 / np.sqrt(E) / u[:, None]),
            "gcn1_b": bf(np.random.standard_normal(H) * 0.1)}


def core(h_enc, adj, gcn1_w, gcn1_b):
    a = f64(adj)
    deg = a.sum(axis=1)
    dis = deg ** -0.5
    xw = mxq(f64(h_enc), 1, "e4m3") @ mxq(f64(gcn1_w), 0, "e4m3")
    y = dis[:, None] * xw
    agg = mxq(a, 1, "e4m3") @ mxq(y, 0, "e4m3")
    return np.maximum(dis[:, None] * agg + f64(gcn1_b), 0.0)


def e4m3fn_bytes(y):
    return np.clip(np.asarray(y, np.float64), -448.0, 448.0).astype(np.float32).astype(ml_dtypes.float8_e4m3fn).view(np.uint8)


def e4m3fn_values(b):
    return np.asarray(b, np.uint8).view(ml_dtypes.float8_e4m3fn).astype(np.float64)


def setup_inputs():
    d = draw0()
    x0 = np.asarray(d['gcn1_w']).astype(np.float64)
    s = (np.max(np.abs(x0), axis=(1,), keepdims=True) / 448.0).astype(np.float32)
    out = {}
    for k, v in d.items():
        if k == 'gcn1_w':
            out['gcn1_w_bytes'] = e4m3fn_bytes(x0 / s.astype(np.float64))
            out['gcn1_w_scale'] = s
        else:
            out[k] = v
    return out


def reference(h_enc, adj, gcn1_w_bytes, gcn1_w_scale, gcn1_b):
    return core(h_enc, adj, e4m3fn_values(gcn1_w_bytes) * gcn1_w_scale.astype(np.float64), gcn1_b)

@@ -1,0 +1,227 @@
+from contextlib import ExitStack
+
+import concourse.mybir as mybir
+from concourse.masks import make_identity
+
+N, E, H = 2048, 512, 256
+FLOPS = 2 * N * E * H + 2 * N * N * H
+
+F32 = mybir.dt.float32
+BF16 = mybir.dt.bfloat16
+U32 = mybir.dt.uint32
+U8 = mybir.dt.uint8
+FP8 = mybir.dt.float8_e4m3fn
+FP8X4 = mybir.dt.float8_e4m3fn_x4
+ALU = mybir.AluOpType
+ACT = mybir.ActivationFunctionType
+
+P = 128
+GROUPS = 4
+TILES = 16
+KIND = "V V V V V V V V S V V S V V S V".split(" ")
+LOADS = "w a0 a1 a2 a3 h0 a4 h1 a5 a6 a7 a8 h2 a9 h3 a10 a11 a12 a13 a14 a15".split(" ")
+ORDER = "wact deg0 wcp deg1 tr0.0 tr0.1 cp0.0 deg2 cp0.1 tr1.0 tr1.1 cp1.0 deg3 cp1.1 tr2.0 tr2.1 cp2.0 htr0.0 wq cp2.1 htr0.1 q0 pow0 tr3.0 hcp0.0 deg4 tr3.1 hcp0.1 cp3.0 htr1.0 q1 htr1.1 cp3.1 hq0 tr4.0 hcp1.0 deg5 tr4.1 hcp1.1 xw0.0 xw0.1 cp4.0 deg6 tr5.0 cp4.1 tr5.1 cp5.0 deg7 tr6.0 cp5.1 tr6.1 deg8 yt0.0 tr7.0 tr7.1 yt0.1 hq1 deg9 pow1 xw1.0 cp6.0 xw1.1 cp6.1 htr2.0 yq0 cp7.0 yt1.0 htr2.1 hcp2.0 yt1.1 htr3.0 hcp2.1 deg10 htr3.1 hcp3.0 tr8.0 deg11 hq2 tr8.1 deg12 xw2.0 xw2.1 deg13 hcp3.1 pow2 deg14 tr9.0 hq3 yt2.0 xw3.0 xw3.1 deg15 cp7.1 yt2.1 pow3 cp8.0 tr9.1 yq1 yt3.0 cp8.1 tr10.0 yt3.1 cp9.0 tr10.1 yq2 cp9.1 tr11.0 yq3 aga0 cp10.0 q2 tr11.1 cp10.1 q3 ag0 tr12.0 cp11.0 st0 aga1 q4 cp11.1 tr12.1 ag1 q5 tr13.0 cp12.0 tr13.1 st1 cp12.1 aga2 q6 tr14.0 rl1 q7 ag2 tr14.1 cp13.0 aga3 st2 cp13.1 q8 aga4 cp14.0 ag3 q9 tr15.0 ag4 cp14.1 st3 tr15.1 aga5 st4 cp15.0 q10 aga6 rl3 q11 ag5 aga7 cp15.1 st5 ag6 aga8 q12 rl5 ag7 aga9 st6 st7 ag8 aga10 q13 rl7 ag9 aga11 st8 st9 ag10 aga12 q14 rl9 ag11 aga13 st10 st11 ag12 aga14 q15 rl11 ag13 st12 ag14 aga15 st13 st14 ag15 rl13 st15 rl15".split(" ")
+
+
+def tile_gcnclassifer_pa_kernel(tc, h_enc, adj, w_bytes, w_scale, b, out):
+    nc = tc.nc
+    h_view = h_enc.rearrange("(g p s) e -> g p s e", p=P, s=4)
+    a_view = adj.rearrange("(g p s) j -> g s p j", p=P, s=4)
+    o_view = out.rearrange("(g p s) h -> g p s h", p=P, s=4)
+
+    with ExitStack() as ctx:
+        keep = ctx.enter_context(tc.tile_pool(name="keep", bufs=1))
+        work = ctx.enter_context(tc.tile_pool(name="work", bufs=3))
+        ordered = ctx.enter_context(tc.tile_pool(name="ordered", bufs=10))
+        tp_pool = ctx.enter_context(tc.psum_pool(name="tp", bufs=4))
+        mm_pool = ctx.enter_context(tc.psum_pool(name="mm", bufs=4))
+        n1_pool = ctx.enter_context(tc.psum_pool(name="n1", bufs=max(1, 0))) if 0 else None
+        ctx.enter_context(tc.manual_schedule())
+
+        a_raw = [keep.tile([P, N], BF16, name=f"a_raw{r}", align_bytes=64) for r in range(TILES)]
+        h_raw = [keep.tile([P, 4 * E], BF16, name=f"h_raw{g}", align_bytes=64) for g in range(GROUPS)]
+        a_ord = {}
+        a_cod = [keep.tile([P, N // 4], U32, name=f"a_cod{r}", align_bytes=64) for r in range(TILES)]
+        a_scl = [keep.tile([P, N // 4], U8, name=f"a_scl{r}", align_bytes=64) for r in range(TILES)]
+        h_cod = [keep.tile([P, 512], U32, name=f"h_cod{g}", align_bytes=64) for g in range(GROUPS)]
+        h_scl = [keep.tile([P, 512], U8, name=f"h_scl{g}", align_bytes=64) for g in range(GROUPS)]
+        y_cod = [keep.tile([P, H], U32, name=f"y_cod{g}", align_bytes=64) for g in range(GROUPS)]
+        y_scl = [keep.tile([P, H], U8, name=f"y_scl{g}", align_bytes=64) for g in range(GROUPS)]
+        w_cod = keep.tile([P, H], U32, name="w_cod", align_bytes=64)
+        w_scl = keep.tile([P, H], U8, name="w_scl", align_bytes=64)
+        w_raw = keep.tile([P, 4 * H], U8, name="w_raw", align_bytes=64)
+        w_sc = keep.tile([P, 4], F32, name="w_sc")
+        w_pl = keep.tile([P, 4, H], BF16, name="w_pl", align_bytes=64)
+        w_grp = keep.tile([P, H, 4], BF16, name="w_grp", align_bytes=64)
+        ident = keep.tile([P, P], F32, name="ident")
+        ident_b = keep.tile([P, P], BF16, name="ident_b")
+        junk = keep.tile([P, 512], BF16, name="junk")
+        ones = keep.tile([P, P], BF16, name="ones")
+        b_row = keep.tile([P, H], BF16, name="b_row")
+        b_all = keep.tile([P, H], F32, name="b_all")
+        deg = keep.tile([P, TILES], F32, name="deg")
+        dis = keep.tile([P, TILES], F32, name="dis")
+        warm = keep.tile([P, 1], F32, name="warm")
+
+        def load_a(r):
+            nc.sync.dma_start(out=a_raw[r][:], in_=a_view[r // 4, r % 4])
+
+        def load_h(g):
+            nc.sync.dma_start(out=h_raw[g][:].rearrange("p (s e) -> p s e", s=4), in_=h_view[g])
+
+        for item in LOADS:
+            if item == "w":
+                nc.sync.dma_start(out=w_raw[:].rearrange("p (t n) -> p t n", t=4), in_=w_bytes.rearrange("(p t) n -> p t n", t=4))
+                nc.sync.dma_start(out=w_sc[:], in_=w_scale.rearrange("(p t) o -> p (t o)", t=4))
+            elif item[0] == "a":
+                load_a(int(item[1:]))
+            else:
+                load_h(int(item[1:]))
+
+        make_identity(nc, ident[:])
+        nc.gpsimd.memset(b_row[:], 0.0)
+        nc.gpsimd.dma_start(out=b_row[0:1, :], in_=b.rearrange("(o n) -> o n", o=1))
+        if any(k[0] == "P" for k in KIND):
+            make_identity(nc, ident_b[:])
+        nc.gpsimd.memset(ones[:], 1.0)
+        nc.gpsimd.memset(warm[:], 1.0)
+        nc.scalar.activation(warm[:], warm[:], ACT.Abs_reciprocal_sqrt)
+
+        tiles = {}
+
+        def do_deg(r):
+            col = deg[:, r : r + 1]
+            if KIND[r] == "N":
+                nc.scalar.copy(out=col, in_=tiles["n1", r][:, 0:1])
+                return
+            if KIND[r] == "PV":
+                nc.vector.tensor_reduce(out=col, in_=tiles["pm", r][:], axis=mybir.AxisListType.X, op=ALU.add)
+                return
+            if KIND[r] == "PS":
+                nc.scalar.activation(junk[:], tiles["pm", r][:], ACT.Copy, accum_out=col)
+                return
+            src = a_raw[r][:].rearrange("p (n u e) -> p u n e", u=2, e=2)
+            a_ord[r] = ordered.tile([P, N], BF16, name="a_ord", align_bytes=64)
+            dst = a_ord[r][:].rearrange("p (u n e) -> p u n e", u=2, e=2)
+            if KIND[r] == "S":
+                nc.scalar.activation(dst, src, ACT.Copy, accum_out=col)
+            else:
+                nc.vector.tensor_scalar(out=dst, in0=src, scalar1=1.0, scalar2=None, op0=ALU.mult, op1=ALU.add, accum_out=col)
+
+        def do_pm(r):
+            bank = n1_pool.tile([P, 512], F32, name="n1b")
+            tiles["pm", r] = bank
+            for c in range(4):
+                nc.tensor.matmul(bank[:], lhsT=ident_b[:], rhs=a_raw[r][:, 512 * c : 512 * c + 512], start=(c == 0), stop=(c == 3))
+
+        def do_n1(r):
+            bank = n1_pool.tile([P, 512], F32, name="n1b")
+            tiles["n1", r] = bank
+            for i in range(16):
+                nc.tensor.matmul(bank[:, 0:1], lhsT=tiles["a_grp", r][:, 512 * (i // 4) + i % 4 : 512 * (i // 4) + 512 : 4], rhs=ones[:, 0:1], start=(i == 0), stop=(i == 15))
+
+        def do_pow(g):
+            cols = slice(4 * g, 4 * g + 4)
+            nc.scalar.activation(dis[:, cols], deg[:, cols], ACT.Abs_reciprocal_sqrt)
+
+        def do_tr(r, half):
+            bank = tp_pool.tile([P, 512], F32, name="bank")
+            tiles["tp", r, half] = bank
+            raw = KIND[r][0] in "NP"
+            words = a_raw[r][:].bitcast(F32) if raw else a_ord[r][:].bitcast(F32)
+            for c2 in range(2):
+                for u in range(2):
+                    c = 2 * half + c2
+                    src = words[:, 256 * c + u : 256 * c + 256 : 2] if raw else words[:, 512 * u + 128 * c : 512 * u + 128 * c + 128]
+                    nc.tensor.transpose(bank[:, 256 * c2 + 128 * u : 256 * c2 + 128 * u + 128], src, ident[:])
+
+        def do_cp(r, half):
+            if ("a_grp", r) not in tiles:
+                if KIND[r] in "VS":
+                    tiles["a_grp", r] = a_raw[r]
+                else:
+                    tiles["a_grp", r] = work.tile([P, N], BF16, name="a_grp", align_bytes=64)
+            nc.scalar.copy(out=tiles["a_grp", r][:].bitcast(F32)[:, 512 * half : 512 * half + 512].rearrange("p (c i u) -> p c i u", c=2, u=2), in_=tiles["tp", r, half][:].rearrange("p (c u i) -> p c i u", c=2, u=2))
+
+        def do_q(r):
+            nc.vector.quantize_mx(out=a_cod[r][:].bitcast(FP8X4), scales=a_scl[r][:], in_=tiles["a_grp", r][:])
+
+        def do_htr(g, half):
+            bank = tp_pool.tile([P, 512], F32, name="bank")
+            tiles["htp", g, half] = bank
+            words = h_raw[g][:].bitcast(F32)
+            for s2 in range(2):
+                for u in range(2):
+                    s = 2 * half + s2
+                    nc.tensor.transpose(bank[:, 256 * s2 + 128 * u : 256 * s2 + 128 * u + 128], words[:, 256 * s + u : 256 * s + 256 : 2], ident[:])
+
+        def do_hcp(g, half):
+            if ("h_grp", g) not in tiles:
+                tiles["h_grp", g] = work.tile([P, 4 * E], BF16, name="h_grp", align_bytes=64)
+            nc.scalar.copy(out=tiles["h_grp", g][:].bitcast(F32)[:, 512 * half : 512 * half + 512].rearrange("p (s j u) -> p s j u", s=2, u=2), in_=tiles["htp", g, half][:].rearrange("p (s u j) -> p s j u", s=2, u=2))
+
+        def do_hq(g):
+            nc.vector.quantize_mx(out=h_cod[g][:].bitcast(FP8X4), scales=h_scl[g][:], in_=tiles["h_grp", g][:])
+
+        def do_xw(g, half):
+            cols = slice(128 * half, 128 * half + 128)
+            bank = mm_pool.tile([P, 512], F32, name="mm")
+            tiles["xw", g, half] = bank
+            for s in range(4):
+                rows = slice(128 * s, 128 * s + 128)
+                nc.tensor.matmul_mx(out=bank[:, rows], lhsT=h_cod[g][:, rows].bitcast(FP8X4), lhsT_scale=h_scl[g][:, rows], rhs=w_cod[:, cols].bitcast(FP8X4), rhs_scale=w_scl[:, cols], start=True, stop=True)
+
+        def do_yt(g, half):
+            if ("y_grp", g) not in tiles:
+                tiles["y_grp", g] = work.tile([P, 4 * H], BF16, name="y_grp", align_bytes=64)
+            nc.vector.tensor_tensor(out=tiles["y_grp", g][:, 512 * half : 512 * half + 512].rearrange("p (n s) -> p n s", s=4), in0=tiles["xw", g, half][:].rearrange("p (s n) -> p n s", s=4), in1=dis[:, 4 * g : 4 * g + 4].unsqueeze(1).to_broadcast([P, 128, 4]), op=ALU.mult)
+
+        def do_yq(g):
+            nc.vector.quantize_mx(out=y_cod[g][:].bitcast(FP8X4), scales=y_scl[g][:], in_=tiles["y_grp", g][:])
+
+        def mx_pass(r, c):
+            rows = slice(128 * c, 128 * c + 128)
+            nc.tensor.matmul_mx(out=tiles["ag", r][:, 0:H], lhsT=a_cod[r][:, rows].bitcast(FP8X4), lhsT_scale=a_scl[r][:, rows], rhs=y_cod[c][:].bitcast(FP8X4), rhs_scale=y_scl[c][:], start=(c == 0), stop=(c == 3))
+
+        def do_aga(r):
+            tiles["ag", r] = mm_pool.tile([P, 512], F32, name="mm")
+            for c in range(3):
+                mx_pass(r, c)
+
+        def do_ag(r):
+            mx_pass(r, 3)
+
+        def do_st(r):
+            i = r % 2
+            if ("sums", r // 2) not in tiles:
+                tiles["sums", r // 2] = work.tile([P, 2 * H], F32, name="sums")
+            nc.vector.scalar_tensor_tensor(out=tiles["sums", r // 2][:, H * i : H * i + H], in0=tiles["ag", r][:, 0:H], scalar=dis[:, r : r + 1], in1=b_all[:], op0=ALU.mult, op1=ALU.add)
+
+        def do_rl(r):
+            pair = r // 2
+            res = work.tile([P, 2 * H], F32, name="res")
+            nc.scalar.activation(res[:], tiles["sums", pair][:], ACT.Relu)
+            nc.sync.dma_start(out=o_view[pair // 2][:, 2 * (pair % 2) : 2 * (pair % 2) + 2, :], in_=res[:].rearrange("p (s n) -> p s n", s=2))
+
+        def do_wact():
+            for t in range(4):
+                nc.scalar.activation(w_pl[:, t, :], w_raw[:, H * t : H * t + H].bitcast(FP8), ACT.Copy, scale=w_sc[:, t : t + 1])
+
+        def do_wcp():
+            nc.scalar.copy(out=w_grp[:], in_=w_pl[:].rearrange("p t n -> p n t"))
+
+        def do_wq():
+            nc.vector.quantize_mx(out=w_cod[:].bitcast(FP8X4), scales=w_scl[:], in_=w_grp[:].rearrange("p n t -> p (n t)"))
+            bank = mm_pool.tile([P, 512], F32, name="mm")
+            nc.tensor.matmul(bank[:, 0:H], lhsT=ones[:], rhs=b_row[:], start=True, stop=True)
+            nc.scalar.copy(out=b_all[:], in_=bank[:, 0:H])
+
+        table = {"wact": do_wact, "wcp": do_wcp, "wq": do_wq, "deg": do_deg, "pm": do_pm, "pow": do_pow, "tr": do_tr, "cp": do_cp, "q": do_q, "htr": do_htr, "hcp": do_hcp, "hq": do_hq, "xw": do_xw, "yt": do_yt, "yq": do_yq, "aga": do_aga, "ag": do_ag, "st": do_st, "rl": do_rl, "n1": do_n1}
+        for token in ORDER:
+            word = token if token.startswith("n1") else token.replace(".", " ")
+            if token.startswith("n1"):
+                do_n1(int(token[2:]))
+                continue
+            names = [n for n in table if word.startswith(n) and all(ch in "0123456789 " for ch in word[len(n) :])]
+            n = names[0]
+            table[n](*[int(v) for v in word[len(n) :].split(" ") if v])

@@ -18,9 +18,10 @@ ACT = mybir.ActivationFunctionType
 P = 128
 GROUPS = 4
 TILES = 16
-KIND = "V V V V V V V V S V V S V V S V".split(" ")
-LOADS = "w a0 a1 a2 a3 h0 a4 h1 a5 a6 a7 a8 h2 a9 h3 a10 a11 a12 a13 a14 a15".split(" ")
-ORDER = "wact deg0 wcp deg1 tr0.0 tr0.1 cp0.0 deg2 cp0.1 tr1.0 tr1.1 cp1.0 deg3 cp1.1 tr2.0 tr2.1 cp2.0 htr0.0 wq cp2.1 htr0.1 q0 pow0 tr3.0 hcp0.0 deg4 tr3.1 hcp0.1 cp3.0 htr1.0 q1 htr1.1 cp3.1 hq0 tr4.0 hcp1.0 deg5 tr4.1 hcp1.1 xw0.0 xw0.1 cp4.0 deg6 tr5.0 cp4.1 tr5.1 cp5.0 deg7 tr6.0 cp5.1 tr6.1 deg8 yt0.0 tr7.0 tr7.1 yt0.1 hq1 deg9 pow1 xw1.0 cp6.0 xw1.1 cp6.1 htr2.0 yq0 cp7.0 yt1.0 htr2.1 hcp2.0 yt1.1 htr3.0 hcp2.1 deg10 htr3.1 hcp3.0 tr8.0 deg11 hq2 tr8.1 deg12 xw2.0 xw2.1 deg13 hcp3.1 pow2 deg14 tr9.0 hq3 yt2.0 xw3.0 xw3.1 deg15 cp7.1 yt2.1 pow3 cp8.0 tr9.1 yq1 yt3.0 cp8.1 tr10.0 yt3.1 cp9.0 tr10.1 yq2 cp9.1 tr11.0 yq3 aga0 cp10.0 q2 tr11.1 cp10.1 q3 ag0 tr12.0 cp11.0 st0 aga1 q4 cp11.1 tr12.1 ag1 q5 tr13.0 cp12.0 tr13.1 st1 cp12.1 aga2 q6 tr14.0 rl1 q7 ag2 tr14.1 cp13.0 aga3 st2 cp13.1 q8 aga4 cp14.0 ag3 q9 tr15.0 ag4 cp14.1 st3 tr15.1 aga5 st4 cp15.0 q10 aga6 rl3 q11 ag5 aga7 cp15.1 st5 ag6 aga8 q12 rl5 ag7 aga9 st6 st7 ag8 aga10 q13 rl7 ag9 aga11 st8 st9 ag10 aga12 q14 rl9 ag11 aga13 st10 st11 ag12 aga14 q15 rl11 ag13 st12 ag14 aga15 st13 st14 ag15 rl13 st15 rl15".split(" ")
+KIND = "V V V V V V V V V V V V V V V V".split(" ")
+YK = "SSSS"
+LOADS = "w a0 a1 a2 a3 h0 a4 h1 a5 a6 a7 a8 a9 h2 a10 a11 h3 a12 a13 a14 a15".split(" ")
+ORDER = "wact deg0 wcp deg1 tr0.0 tr0.1 cp0.0 deg2 tr1.0 cp0.1 tr1.1 cp1.0 deg3 tr2.0 cp1.1 tr2.1 cp2.0 htr0.0 wq pow0 q0 cp2.1 htr0.1 deg4 hcp0.0 tr3.0 tr3.1 hcp0.1 htr1.0 cp3.0 q1 htr1.1 hcp1.0 hq0 tr4.0 hcp1.1 deg5 tr4.1 cp3.1 xw0.0 xw0.1 cp4.0 deg6 tr5.0 ys0.0 tr5.1 ys0.1 deg7 tr6.0 cp4.1 yi0 cp5.0 deg8 tr6.1 pow1 cp5.1 tr7.0 deg9 cp6.0 tr7.1 cp6.1 htr2.0 cp7.0 yq0 htr2.1 deg10 hcp2.0 tr8.0 hcp2.1 tr8.1 deg11 cp7.1 tr9.0 cp8.0 htr3.0 hq1 cp8.1 htr3.1 hq2 pow2 hcp3.0 tr9.1 deg12 hcp3.1 xw1.0 xw1.1 cp9.0 xw2.0 hq3 xw2.1 ys1.0 tr10.0 deg13 ys1.1 tr10.1 tr11.0 ys2.0 yi1 xw3.0 deg14 ys2.1 xw3.1 cp9.1 deg15 cp10.0 yi2 tr11.1 cp10.1 tr12.0 yq1 cp11.0 q2 tr12.1 pow3 cp11.1 tr13.0 yq2 q3 ys3.0 tr13.1 q4 ys3.1 aga0 q5 cp12.0 aga1 yi3 aga2 q6 cp12.1 aga3 cp13.0 q7 tr14.0 cp13.1 q8 tr14.1 tr15.0 cp14.0 yq3 tr15.1 q9 cp14.1 ag0 ag1 q10 cp15.0 ag2 ag3 st0 cp15.1 st1 aga4 st2 rl1 st3 aga5 q11 ag4 rl3 aga6 st4 ag5 aga7 q12 ag6 aga8 st5 ag7 st6 ag8 rl5 st7 aga9 st8 aga10 rl7 q13 ag9 aga11 st9 ag10 aga12 q14 rl9 ag11 aga13 st10 st11 ag12 aga14 q15 rl11 ag13 ag14 st12 aga15 st13 st14 rl13 ag15 st15 rl15".split(" ")
 
 
 def tile_gcnclassifer_pa_kernel(tc, h_enc, adj, w_bytes, w_scale, b, out):
@@ -31,7 +32,7 @@ def tile_gcnclassifer_pa_kernel(tc, h_enc, adj, w_bytes, w_scale, b, out):
 
     with ExitStack() as ctx:
         keep = ctx.enter_context(tc.tile_pool(name="keep", bufs=1))
-        work = ctx.enter_context(tc.tile_pool(name="work", bufs=3))
+        work = ctx.enter_context(tc.tile_pool(name="work", bufs=2))
         ordered = ctx.enter_context(tc.tile_pool(name="ordered", bufs=10))
         tp_pool = ctx.enter_context(tc.psum_pool(name="tp", bufs=4))
         mm_pool = ctx.enter_context(tc.psum_pool(name="mm", bufs=4))
@@ -94,6 +95,9 @@ def tile_gcnclassifer_pa_kernel(tc, h_enc, adj, w_bytes, w_scale, b, out):
             if KIND[r] == "N":
                 nc.scalar.copy(out=col, in_=tiles["n1", r][:, 0:1])
                 return
+            if KIND[r] == "G":
+                nc.vector.tensor_reduce(out=col, in_=tiles["gg", r][:, 0:64], axis=mybir.AxisListType.X, op=ALU.add)
+                return
             if KIND[r] == "PV":
                 nc.vector.tensor_reduce(out=col, in_=tiles["pm", r][:], axis=mybir.AxisListType.X, op=ALU.add)
                 return
@@ -107,6 +111,19 @@ def tile_gcnclassifer_pa_kernel(tc, h_enc, adj, w_bytes, w_scale, b, out):
                 nc.scalar.activation(dst, src, ACT.Copy, accum_out=col)
             else:
                 nc.vector.tensor_scalar(out=dst, in0=src, scalar1=1.0, scalar2=None, op0=ALU.mult, op1=ALU.add, accum_out=col)
+
+        def do_gg(r):
+            part = work.tile([P, 1024], F32, name="part", align_bytes=64)
+            tiles["gg", r] = part
+            for c in range(4):
+                cols = slice(256 * c, 256 * c + 256)
+                nc.gpsimd.tensor_tensor(out=part[:, cols], in0=a_raw[r][:, cols], in1=a_raw[r][:, 1024 + 256 * c : 1280 + 256 * c], op=ALU.add)
+            width = 512
+            while width >= 64:
+                for lo in range(0, width, 256):
+                    hi = min(width, lo + 256)
+                    nc.gpsimd.tensor_tensor(out=part[:, lo:hi], in0=part[:, lo:hi], in1=part[:, width + lo : width + hi], op=ALU.add)
+                width = width // 2
 
         def do_pm(r):
             bank = n1_pool.tile([P, 512], F32, name="n1b")
@@ -127,7 +144,7 @@ def tile_gcnclassifer_pa_kernel(tc, h_enc, adj, w_bytes, w_scale, b, out):
         def do_tr(r, half):
             bank = tp_pool.tile([P, 512], F32, name="bank")
             tiles["tp", r, half] = bank
-            raw = KIND[r][0] in "NP"
+            raw = KIND[r][0] in "NPG"
             words = a_raw[r][:].bitcast(F32) if raw else a_ord[r][:].bitcast(F32)
             for c2 in range(2):
                 for u in range(2):
@@ -164,6 +181,13 @@ def tile_gcnclassifer_pa_kernel(tc, h_enc, adj, w_bytes, w_scale, b, out):
             nc.vector.quantize_mx(out=h_cod[g][:].bitcast(FP8X4), scales=h_scl[g][:], in_=tiles["h_grp", g][:])
 
         def do_xw(g, half):
+            if YK[g] == "S":
+                bank = mm_pool.tile([P, 512], F32, name="mm")
+                tiles["xw", g, half] = bank
+                for s in range(2):
+                    rows = slice(128 * (2 * half + s), 128 * (2 * half + s) + 128)
+                    nc.tensor.matmul_mx(out=bank[:, H * s : H * s + H], lhsT=h_cod[g][:, rows].bitcast(FP8X4), lhsT_scale=h_scl[g][:, rows], rhs=w_cod[:].bitcast(FP8X4), rhs_scale=w_scl[:], start=True, stop=True)
+                return
             cols = slice(128 * half, 128 * half + 128)
             bank = mm_pool.tile([P, 512], F32, name="mm")
             tiles["xw", g, half] = bank
@@ -175,6 +199,17 @@ def tile_gcnclassifer_pa_kernel(tc, h_enc, adj, w_bytes, w_scale, b, out):
             if ("y_grp", g) not in tiles:
                 tiles["y_grp", g] = work.tile([P, 4 * H], BF16, name="y_grp", align_bytes=64)
             nc.vector.tensor_tensor(out=tiles["y_grp", g][:, 512 * half : 512 * half + 512].rearrange("p (n s) -> p n s", s=4), in0=tiles["xw", g, half][:].rearrange("p (s n) -> p n s", s=4), in1=dis[:, 4 * g : 4 * g + 4].unsqueeze(1).to_broadcast([P, 128, 4]), op=ALU.mult)
+
+        def do_ys(g, half):
+            if ("y_pl", g) not in tiles:
+                tiles["y_pl", g] = work.tile([P, 4 * H], BF16, name="y_pl", align_bytes=64)
+            for s in range(2):
+                col = 2 * half + s
+                nc.scalar.activation(tiles["y_pl", g][:, H * col : H * col + H], tiles["xw", g, half][:, H * s : H * s + H], ACT.Copy, scale=dis[:, 4 * g + col : 4 * g + col + 1])
+
+        def do_yi(g):
+            tiles["y_grp", g] = work.tile([P, 4 * H], BF16, name="y_grp", align_bytes=64)
+            nc.gpsimd.tensor_scalar(out=tiles["y_grp", g][:].rearrange("p (n s) -> p n s", s=4), in0=tiles["y_pl", g][:].rearrange("p (s n) -> p n s", s=4), scalar1=1.0, scalar2=0.0, op0=ALU.mult, op1=ALU.add)
 
         def do_yq(g):
             nc.vector.quantize_mx(out=y_cod[g][:].bitcast(FP8X4), scales=y_scl[g][:], in_=tiles["y_grp", g][:])
@@ -216,7 +251,7 @@ def tile_gcnclassifer_pa_kernel(tc, h_enc, adj, w_bytes, w_scale, b, out):
             nc.tensor.matmul(bank[:, 0:H], lhsT=ones[:], rhs=b_row[:], start=True, stop=True)
             nc.scalar.copy(out=b_all[:], in_=bank[:, 0:H])
 
-        table = {"wact": do_wact, "wcp": do_wcp, "wq": do_wq, "deg": do_deg, "pm": do_pm, "pow": do_pow, "tr": do_tr, "cp": do_cp, "q": do_q, "htr": do_htr, "hcp": do_hcp, "hq": do_hq, "xw": do_xw, "yt": do_yt, "yq": do_yq, "aga": do_aga, "ag": do_ag, "st": do_st, "rl": do_rl, "n1": do_n1}
+        table = {"wact": do_wact, "wcp": do_wcp, "wq": do_wq, "deg": do_deg, "pm": do_pm, "pow": do_pow, "tr": do_tr, "cp": do_cp, "q": do_q, "htr": do_htr, "hcp": do_hcp, "hq": do_hq, "xw": do_xw, "yt": do_yt, "yq": do_yq, "ys": do_ys, "yi": do_yi, "gg": do_gg, "aga": do_aga, "ag": do_ag, "st": do_st, "rl": do_rl, "n1": do_n1}
         for token in ORDER:
             word = token if token.startswith("n1") else token.replace(".", " ")
             if token.startswith("n1"):

@@ -18,10 +18,10 @@ ACT = mybir.ActivationFunctionType
 P = 128
 GROUPS = 4
 TILES = 16
-KIND = "V V V V V V V V V V V V V V V V".split(" ")
-YK = "SSSS"
-LOADS = "w a0 a1 a2 a3 h0 a4 h1 a5 a6 a7 a8 a9 h2 a10 a11 h3 a12 a13 a14 a15".split(" ")
-ORDER = "wact deg0 wcp deg1 tr0.0 tr0.1 cp0.0 deg2 tr1.0 cp0.1 tr1.1 cp1.0 deg3 tr2.0 cp1.1 tr2.1 cp2.0 htr0.0 wq pow0 q0 cp2.1 htr0.1 deg4 hcp0.0 tr3.0 tr3.1 hcp0.1 htr1.0 cp3.0 q1 htr1.1 hcp1.0 hq0 tr4.0 hcp1.1 deg5 tr4.1 cp3.1 xw0.0 xw0.1 cp4.0 deg6 tr5.0 ys0.0 tr5.1 ys0.1 deg7 tr6.0 cp4.1 yi0 cp5.0 deg8 tr6.1 pow1 cp5.1 tr7.0 deg9 cp6.0 tr7.1 cp6.1 htr2.0 cp7.0 yq0 htr2.1 deg10 hcp2.0 tr8.0 hcp2.1 tr8.1 deg11 cp7.1 tr9.0 cp8.0 htr3.0 hq1 cp8.1 htr3.1 hq2 pow2 hcp3.0 tr9.1 deg12 hcp3.1 xw1.0 xw1.1 cp9.0 xw2.0 hq3 xw2.1 ys1.0 tr10.0 deg13 ys1.1 tr10.1 tr11.0 ys2.0 yi1 xw3.0 deg14 ys2.1 xw3.1 cp9.1 deg15 cp10.0 yi2 tr11.1 cp10.1 tr12.0 yq1 cp11.0 q2 tr12.1 pow3 cp11.1 tr13.0 yq2 q3 ys3.0 tr13.1 q4 ys3.1 aga0 q5 cp12.0 aga1 yi3 aga2 q6 cp12.1 aga3 cp13.0 q7 tr14.0 cp13.1 q8 tr14.1 tr15.0 cp14.0 yq3 tr15.1 q9 cp14.1 ag0 ag1 q10 cp15.0 ag2 ag3 st0 cp15.1 st1 aga4 st2 rl1 st3 aga5 q11 ag4 rl3 aga6 st4 ag5 aga7 q12 ag6 aga8 st5 ag7 st6 ag8 rl5 st7 aga9 st8 aga10 rl7 q13 ag9 aga11 st9 ag10 aga12 q14 rl9 ag11 aga13 st10 st11 ag12 aga14 q15 rl11 ag13 ag14 st12 aga15 st13 st14 rl13 ag15 st15 rl15".split(" ")
+KIND = "V V V P V V P V G V V V G S P V".split(" ")
+YK = "VVVV"
+LOADS = "a0 b0 w a1 a2 a3 a4 a5 a6 h0 a7 a8 h1 a9 h2 h3 a10 a11 a12 a13 a14 a15".split(" ")
+ORDER = "dega0 wact deg0 tr0.0 tr0.1 deg1 cp0.0 biasm wcp deg2 tr1.0 tr1.1 pm3 biasc wq cp0.1 deg4 cp1.0 tr2.0 cp1.1 tr2.1 tr3.0 q0 cp2.0 tr3.1 q1 cp2.1 pm6 deg3 cp3.0 deg5 pow0 cp3.1 htr0.0 q2 htr0.1 hcp0.0 deg6 tr4.0 deg7 hcp0.1 tr4.1 gg8 tr5.0 cp4.0 tr5.1 hq0 cp4.1 tr6.0 q3 pow1 cp5.0 htr1.0 q4 cp5.1 xw0.0 deg9 xw0.1 cp6.0 htr1.1 hcp1.0 htr2.0 yt0.0 hcp1.1 htr2.1 yt0.1 hcp2.0 htr3.0 hq1 hcp2.1 htr3.1 yq0 tr6.1 hcp3.0 deg10 tr7.0 hcp3.1 tr7.1 cp6.1 xw1.0 hq2 xw1.1 cp7.0 gg12 hq3 tr8.0 cp7.1 deg8 tr8.1 deg11 cp8.0 tr9.0 cp8.1 tr9.1 pm14 yt1.0 cp9.0 yt1.1 pow2 cp9.1 deg15 tr10.0 deg13 tr10.1 tr11.0 yq1 tr11.1 deg14 xw2.0 q5 xw2.1 yt2.0 xw3.0 cp10.0 xw3.1 yt2.1 cp10.1 tr12.0 deg12 cp11.0 q6 tr12.1 pow3 yq2 cp11.1 tr13.0 q7 aga0 cp12.0 yt3.0 aga1 cp12.1 tr13.1 yt3.1 cp13.0 tr14.0 q8 cp13.1 tr14.1 yq3 cp14.0 tr15.0 q9 tr15.1 cp14.1 q10 ag0 ag1 cp15.0 aga2 q11 aga3 cp15.1 st0 ag2 st1 ag3 aga4 st2 rl1 aga5 st3 q12 ag4 aga6 rl3 st4 ag5 aga7 q13 ag6 aga8 st5 ag7 st6 ag8 rl5 aga9 st7 aga10 st8 rl7 q14 ag9 aga11 st9 ag10 aga12 q15 rl9 ag11 aga13 st10 ag12 st11 ag13 aga14 st12 rl11 st13 aga15 ag14 rl13 ag15 st14 st15 rs14 rs15".split(" ")
 
 
 def tile_gcnclassifer_pa_kernel(tc, h_enc, adj, w_bytes, w_scale, b, out):
@@ -34,6 +34,7 @@ def tile_gcnclassifer_pa_kernel(tc, h_enc, adj, w_bytes, w_scale, b, out):
         keep = ctx.enter_context(tc.tile_pool(name="keep", bufs=1))
         work = ctx.enter_context(tc.tile_pool(name="work", bufs=2))
         ordered = ctx.enter_context(tc.tile_pool(name="ordered", bufs=10))
+        tail = ctx.enter_context(tc.tile_pool(name="tail", bufs=4))
         tp_pool = ctx.enter_context(tc.psum_pool(name="tp", bufs=4))
         mm_pool = ctx.enter_context(tc.psum_pool(name="mm", bufs=4))
         n1_pool = ctx.enter_context(tc.psum_pool(name="n1", bufs=max(1, 0))) if 0 else None
@@ -56,12 +57,12 @@ def tile_gcnclassifer_pa_kernel(tc, h_enc, adj, w_bytes, w_scale, b, out):
         w_grp = keep.tile([P, H, 4], BF16, name="w_grp", align_bytes=64)
         ident = keep.tile([P, P], F32, name="ident")
         ident_b = keep.tile([P, P], BF16, name="ident_b")
-        junk = keep.tile([P, 512], BF16, name="junk")
         ones = keep.tile([P, P], BF16, name="ones")
         b_row = keep.tile([P, H], BF16, name="b_row")
         b_all = keep.tile([P, H], F32, name="b_all")
         deg = keep.tile([P, TILES], F32, name="deg")
         dis = keep.tile([P, TILES], F32, name="dis")
+        part_deg = keep.tile([P, 1], F32, name="part_deg")
         warm = keep.tile([P, 1], F32, name="warm")
 
         def load_a(r):
@@ -71,7 +72,10 @@ def tile_gcnclassifer_pa_kernel(tc, h_enc, adj, w_bytes, w_scale, b, out):
             nc.sync.dma_start(out=h_raw[g][:].rearrange("p (s e) -> p s e", s=4), in_=h_view[g])
 
         for item in LOADS:
-            if item == "w":
+            if item in ("a0", "b0"):
+                half = slice(0, 1024) if item == "a0" else slice(1024, 2048)
+                nc.sync.dma_start(out=a_raw[0][:, half], in_=a_view[0, 0][:, half])
+            elif item == "w":
                 nc.sync.dma_start(out=w_raw[:].rearrange("p (t n) -> p t n", t=4), in_=w_bytes.rearrange("(p t) n -> p t n", t=4))
                 nc.sync.dma_start(out=w_sc[:], in_=w_scale.rearrange("(p t) o -> p (t o)", t=4))
             elif item[0] == "a":
@@ -82,13 +86,22 @@ def tile_gcnclassifer_pa_kernel(tc, h_enc, adj, w_bytes, w_scale, b, out):
         make_identity(nc, ident[:])
         nc.gpsimd.memset(b_row[:], 0.0)
         nc.gpsimd.dma_start(out=b_row[0:1, :], in_=b.rearrange("(o n) -> o n", o=1))
-        if any(k[0] == "P" for k in KIND):
+        if any(k == "P" for k in KIND):
             make_identity(nc, ident_b[:])
         nc.gpsimd.memset(ones[:], 1.0)
         nc.gpsimd.memset(warm[:], 1.0)
         nc.scalar.activation(warm[:], warm[:], ACT.Abs_reciprocal_sqrt)
 
         tiles = {}
+
+        def half_degree(half, start, col):
+            src = a_raw[0][:, 1024 * half : 1024 * half + 1024].rearrange("p (n u e) -> p u n e", u=2, e=2)
+            dst = a_ord[0][:].rearrange("p (u n e) -> p u n e", u=2, e=2)[:, :, 256 * half : 256 * half + 256, :]
+            nc.vector.tensor_scalar(out=dst, in0=src, scalar1=1.0, scalar2=start, op0=ALU.mult, op1=ALU.add, accum_out=col)
+
+        def do_dega(r):
+            a_ord[0] = ordered.tile([P, N], BF16, name="a_ord", align_bytes=64)
+            half_degree(0, None, part_deg[:])
 
         def do_deg(r):
             col = deg[:, r : r + 1]
@@ -98,11 +111,11 @@ def tile_gcnclassifer_pa_kernel(tc, h_enc, adj, w_bytes, w_scale, b, out):
             if KIND[r] == "G":
                 nc.vector.tensor_reduce(out=col, in_=tiles["gg", r][:, 0:64], axis=mybir.AxisListType.X, op=ALU.add)
                 return
-            if KIND[r] == "PV":
-                nc.vector.tensor_reduce(out=col, in_=tiles["pm", r][:], axis=mybir.AxisListType.X, op=ALU.add)
+            if KIND[r] == "P":
+                nc.vector.tensor_reduce(out=col, in_=tiles["pm", r][:, 0:P], axis=mybir.AxisListType.X, op=ALU.add)
                 return
-            if KIND[r] == "PS":
-                nc.scalar.activation(junk[:], tiles["pm", r][:], ACT.Copy, accum_out=col)
+            if r == 0:
+                half_degree(1, part_deg[:], col)
                 return
             src = a_raw[r][:].rearrange("p (n u e) -> p u n e", u=2, e=2)
             a_ord[r] = ordered.tile([P, N], BF16, name="a_ord", align_bytes=64)
@@ -126,10 +139,10 @@ def tile_gcnclassifer_pa_kernel(tc, h_enc, adj, w_bytes, w_scale, b, out):
                 width = width // 2
 
         def do_pm(r):
-            bank = n1_pool.tile([P, 512], F32, name="n1b")
+            bank = mm_pool.tile([P, 512], F32, name="mm")
             tiles["pm", r] = bank
-            for c in range(4):
-                nc.tensor.matmul(bank[:], lhsT=ident_b[:], rhs=a_raw[r][:, 512 * c : 512 * c + 512], start=(c == 0), stop=(c == 3))
+            for c in range(16):
+                nc.tensor.matmul(bank[:, 0:P], lhsT=ident_b[:], rhs=a_raw[r][:, P * c : P * c + P], start=(c == 0), stop=(c == 15))
 
         def do_n1(r):
             bank = n1_pool.tile([P, 512], F32, name="n1b")
@@ -229,12 +242,12 @@ def tile_gcnclassifer_pa_kernel(tc, h_enc, adj, w_bytes, w_scale, b, out):
         def do_st(r):
             i = r % 2
             if ("sums", r // 2) not in tiles:
-                tiles["sums", r // 2] = work.tile([P, 2 * H], F32, name="sums")
+                tiles["sums", r // 2] = tail.tile([P, 2 * H], F32, name="sums")
             nc.vector.scalar_tensor_tensor(out=tiles["sums", r // 2][:, H * i : H * i + H], in0=tiles["ag", r][:, 0:H], scalar=dis[:, r : r + 1], in1=b_all[:], op0=ALU.mult, op1=ALU.add)
 
         def do_rl(r):
             pair = r // 2
-            res = work.tile([P, 2 * H], F32, name="res")
+            res = tail.tile([P, 2 * H], F32, name="res")
             nc.scalar.activation(res[:], tiles["sums", pair][:], ACT.Relu)
             nc.sync.dma_start(out=o_view[pair // 2][:, 2 * (pair % 2) : 2 * (pair % 2) + 2, :], in_=res[:].rearrange("p (s n) -> p s n", s=2))
 
@@ -247,11 +260,23 @@ def tile_gcnclassifer_pa_kernel(tc, h_enc, adj, w_bytes, w_scale, b, out):
 
         def do_wq():
             nc.vector.quantize_mx(out=w_cod[:].bitcast(FP8X4), scales=w_scl[:], in_=w_grp[:].rearrange("p n t -> p (n t)"))
-            bank = mm_pool.tile([P, 512], F32, name="mm")
-            nc.tensor.matmul(bank[:, 0:H], lhsT=ones[:], rhs=b_row[:], start=True, stop=True)
-            nc.scalar.copy(out=b_all[:], in_=bank[:, 0:H])
 
-        table = {"wact": do_wact, "wcp": do_wcp, "wq": do_wq, "deg": do_deg, "pm": do_pm, "pow": do_pow, "tr": do_tr, "cp": do_cp, "q": do_q, "htr": do_htr, "hcp": do_hcp, "hq": do_hq, "xw": do_xw, "yt": do_yt, "yq": do_yq, "ys": do_ys, "yi": do_yi, "gg": do_gg, "aga": do_aga, "ag": do_ag, "st": do_st, "rl": do_rl, "n1": do_n1}
+        def do_biasm():
+            tiles["bias"] = mm_pool.tile([P, 512], F32, name="mm")
+            nc.tensor.matmul(tiles["bias"][:, 0:H], lhsT=ones[:], rhs=b_row[:], start=True, stop=True)
+
+        def do_biasc():
+            nc.scalar.copy(out=b_all[:], in_=tiles["bias"][:, 0:H])
+
+        def do_rs(r):
+            i = r % 2
+            if ("res", r // 2) not in tiles:
+                tiles["res", r // 2] = tail.tile([P, 2 * H], F32, name="res")
+            res = tiles["res", r // 2]
+            nc.scalar.activation(res[:, H * i : H * i + H], tiles["sums", r // 2][:, H * i : H * i + H], ACT.Relu)
+            nc.sync.dma_start(out=o_view[r // 4][:, r % 4, :], in_=res[:, H * i : H * i + H])
+
+        table = {"wact": do_wact, "wcp": do_wcp, "wq": do_wq, "deg": do_deg, "pm": do_pm, "pow": do_pow, "tr": do_tr, "cp": do_cp, "q": do_q, "htr": do_htr, "hcp": do_hcp, "hq": do_hq, "xw": do_xw, "yt": do_yt, "yq": do_yq, "ys": do_ys, "yi": do_yi, "gg": do_gg, "dega": do_dega, "biasm": do_biasm, "biasc": do_biasc, "rs": do_rs, "aga": do_aga, "ag": do_ag, "st": do_st, "rl": do_rl, "n1": do_n1}
         for token in ORDER:
             word = token if token.startswith("n1") else token.replace(".", " ")
             if token.startswith("n1"):

@@ -18,10 +18,10 @@ ACT = mybir.ActivationFunctionType
 P = 128
 GROUPS = 4
 TILES = 16
-KIND = "V V V P V V P V G V V V G S P V".split(" ")
+KIND = "V V V V V G V V S G P V G V V P".split(" ")
 YK = "VVVV"
-LOADS = "a0 b0 w a1 a2 a3 a4 a5 a6 h0 a7 a8 h1 a9 h2 h3 a10 a11 a12 a13 a14 a15".split(" ")
-ORDER = "dega0 wact deg0 tr0.0 tr0.1 deg1 cp0.0 biasm wcp deg2 tr1.0 tr1.1 pm3 biasc wq cp0.1 deg4 cp1.0 tr2.0 cp1.1 tr2.1 tr3.0 q0 cp2.0 tr3.1 q1 cp2.1 pm6 deg3 cp3.0 deg5 pow0 cp3.1 htr0.0 q2 htr0.1 hcp0.0 deg6 tr4.0 deg7 hcp0.1 tr4.1 gg8 tr5.0 cp4.0 tr5.1 hq0 cp4.1 tr6.0 q3 pow1 cp5.0 htr1.0 q4 cp5.1 xw0.0 deg9 xw0.1 cp6.0 htr1.1 hcp1.0 htr2.0 yt0.0 hcp1.1 htr2.1 yt0.1 hcp2.0 htr3.0 hq1 hcp2.1 htr3.1 yq0 tr6.1 hcp3.0 deg10 tr7.0 hcp3.1 tr7.1 cp6.1 xw1.0 hq2 xw1.1 cp7.0 gg12 hq3 tr8.0 cp7.1 deg8 tr8.1 deg11 cp8.0 tr9.0 cp8.1 tr9.1 pm14 yt1.0 cp9.0 yt1.1 pow2 cp9.1 deg15 tr10.0 deg13 tr10.1 tr11.0 yq1 tr11.1 deg14 xw2.0 q5 xw2.1 yt2.0 xw3.0 cp10.0 xw3.1 yt2.1 cp10.1 tr12.0 deg12 cp11.0 q6 tr12.1 pow3 yq2 cp11.1 tr13.0 q7 aga0 cp12.0 yt3.0 aga1 cp12.1 tr13.1 yt3.1 cp13.0 tr14.0 q8 cp13.1 tr14.1 yq3 cp14.0 tr15.0 q9 tr15.1 cp14.1 q10 ag0 ag1 cp15.0 aga2 q11 aga3 cp15.1 st0 ag2 st1 ag3 aga4 st2 rl1 aga5 st3 q12 ag4 aga6 rl3 st4 ag5 aga7 q13 ag6 aga8 st5 ag7 st6 ag8 rl5 aga9 st7 aga10 st8 rl7 q14 ag9 aga11 st9 ag10 aga12 q15 rl9 ag11 aga13 st10 ag12 st11 ag13 aga14 st12 rl11 st13 aga15 ag14 rl13 ag15 st14 st15 rs14 rs15".split(" ")
+LOADS = "a0 b0 w a1 a2 a3 a4 a5 h0 a6 h1 a7 a8 a9 h2 a10 a11 a12 h3 a13 a14 a15".split(" ")
+ORDER = "dega0 wact deg0 tr0.0 tr0.1 deg1 cp0.0 wcp deg2 tr1.0 tr1.1 cp0.1 deg3 tr2.0 cp1.0 tr2.1 cp1.1 q0 tr3.0 pow0 wq cp2.0 tr3.1 deg4 gg5 tr5.0 cp2.1 tr5.1 cp3.0 q1 htr0.0 cp3.1 htr0.1 q2 hcp0.0 tr4.0 deg6 hcp0.1 tr4.1 cp4.0 htr1.0 hq0 cp4.1 htr1.1 q3 hcp1.0 tr6.0 deg7 tr6.1 hcp1.1 xw0.0 cp5.0 xw0.1 yt0.0 cp5.1 biasm tr7.0 yt0.1 cp6.0 tr7.1 gg9 hq1 biasc tr9.0 cp6.1 yq0 tr9.1 deg5 cp7.0 q4 htr2.0 pow1 cp7.1 q5 htr2.1 hcp2.0 pm10 q6 hcp2.1 q7 cp9.0 deg11 tr10.0 cp9.1 tr10.1 cp10.0 tr12.0 hq2 cp10.1 htr3.0 deg10 q9 cp12.0 htr3.1 q10 hcp3.0 tr11.0 tr11.1 deg13 hcp3.1 gg12 tr12.1 cp11.0 xw1.0 hq3 cp11.1 xw1.1 xw2.0 yt1.0 cp12.1 xw2.1 xw3.0 yt1.1 deg8 xw3.1 pm15 deg9 deg14 tr13.0 yq1 tr13.1 deg15 q11 pow2 tr8.0 cp13.0 tr8.1 yt2.0 cp8.0 tr14.0 yt2.1 cp8.1 tr14.1 q12 tr15.0 cp13.1 yq2 tr15.1 cp14.0 deg12 q8 aga0 pow3 cp14.1 q13 aga1 cp15.0 aga2 yt3.0 aga3 cp15.1 yt3.1 aga4 aga5 q14 aga6 yq3 aga7 q15 ag0 ag1 ag2 st0 ag3 ag4 ag5 st1 ag6 ag7 st2 aga8 rl1 st3 aga9 st4 ag8 rl3 st5 aga10 st6 ag9 aga11 rl5 st7 st8 ag10 aga12 rl7 st9 ag11 st10 aga13 rl9 st11 ag12 aga14 st12 rl11 ag13 aga15 st13 ag14 ag15 st14 rl13 st15 rs14 rs15".split(" ")
 
 
 def tile_gcnclassifer_pa_kernel(tc, h_enc, adj, w_bytes, w_scale, b, out):
@@ -35,9 +35,7 @@ def tile_gcnclassifer_pa_kernel(tc, h_enc, adj, w_bytes, w_scale, b, out):
         work = ctx.enter_context(tc.tile_pool(name="work", bufs=2))
         ordered = ctx.enter_context(tc.tile_pool(name="ordered", bufs=10))
         tail = ctx.enter_context(tc.tile_pool(name="tail", bufs=4))
-        tp_pool = ctx.enter_context(tc.psum_pool(name="tp", bufs=4))
-        mm_pool = ctx.enter_context(tc.psum_pool(name="mm", bufs=4))
-        n1_pool = ctx.enter_context(tc.psum_pool(name="n1", bufs=max(1, 0))) if 0 else None
+        tp_pool = ctx.enter_context(tc.psum_pool(name="tp", bufs=8))
         ctx.enter_context(tc.manual_schedule())
 
         a_raw = [keep.tile([P, N], BF16, name=f"a_raw{r}", align_bytes=64) for r in range(TILES)]
@@ -71,25 +69,29 @@ def tile_gcnclassifer_pa_kernel(tc, h_enc, adj, w_bytes, w_scale, b, out):
         def load_h(g):
             nc.sync.dma_start(out=h_raw[g][:].rearrange("p (s e) -> p s e", s=4), in_=h_view[g])
 
+        nc.vector.memset(b_row[:], 0.0)
         for item in LOADS:
+            if item == "a3":
+                nc.sync.dma_start(out=b_row[0:1, :], in_=b.rearrange("(o n) -> o n", o=1))
             if item in ("a0", "b0"):
                 half = slice(0, 1024) if item == "a0" else slice(1024, 2048)
                 nc.sync.dma_start(out=a_raw[0][:, half], in_=a_view[0, 0][:, half])
             elif item == "w":
                 nc.sync.dma_start(out=w_raw[:].rearrange("p (t n) -> p t n", t=4), in_=w_bytes.rearrange("(p t) n -> p t n", t=4))
                 nc.sync.dma_start(out=w_sc[:], in_=w_scale.rearrange("(p t) o -> p (t o)", t=4))
+            elif item[0] == "p":
+                load_a(int(item[1:]))
+                load_a(int(item[1:]) + 1)
             elif item[0] == "a":
                 load_a(int(item[1:]))
             else:
                 load_h(int(item[1:]))
 
+        nc.vector.memset(warm[:], 1.0)
         make_identity(nc, ident[:])
-        nc.gpsimd.memset(b_row[:], 0.0)
-        nc.gpsimd.dma_start(out=b_row[0:1, :], in_=b.rearrange("(o n) -> o n", o=1))
+        nc.vector.memset(ones[:], 1.0)
         if any(k == "P" for k in KIND):
             make_identity(nc, ident_b[:])
-        nc.gpsimd.memset(ones[:], 1.0)
-        nc.gpsimd.memset(warm[:], 1.0)
         nc.scalar.activation(warm[:], warm[:], ACT.Abs_reciprocal_sqrt)
 
         tiles = {}
@@ -105,9 +107,6 @@ def tile_gcnclassifer_pa_kernel(tc, h_enc, adj, w_bytes, w_scale, b, out):
 
         def do_deg(r):
             col = deg[:, r : r + 1]
-            if KIND[r] == "N":
-                nc.scalar.copy(out=col, in_=tiles["n1", r][:, 0:1])
-                return
             if KIND[r] == "G":
                 nc.vector.tensor_reduce(out=col, in_=tiles["gg", r][:, 0:64], axis=mybir.AxisListType.X, op=ALU.add)
                 return
@@ -139,16 +138,10 @@ def tile_gcnclassifer_pa_kernel(tc, h_enc, adj, w_bytes, w_scale, b, out):
                 width = width // 2
 
         def do_pm(r):
-            bank = mm_pool.tile([P, 512], F32, name="mm")
+            bank = tp_pool.tile([P, 512], F32, name="bank")
             tiles["pm", r] = bank
             for c in range(16):
                 nc.tensor.matmul(bank[:, 0:P], lhsT=ident_b[:], rhs=a_raw[r][:, P * c : P * c + P], start=(c == 0), stop=(c == 15))
-
-        def do_n1(r):
-            bank = n1_pool.tile([P, 512], F32, name="n1b")
-            tiles["n1", r] = bank
-            for i in range(16):
-                nc.tensor.matmul(bank[:, 0:1], lhsT=tiles["a_grp", r][:, 512 * (i // 4) + i % 4 : 512 * (i // 4) + 512 : 4], rhs=ones[:, 0:1], start=(i == 0), stop=(i == 15))
 
         def do_pow(g):
             cols = slice(4 * g, 4 * g + 4)
@@ -195,14 +188,14 @@ def tile_gcnclassifer_pa_kernel(tc, h_enc, adj, w_bytes, w_scale, b, out):
 
         def do_xw(g, half):
             if YK[g] == "S":
-                bank = mm_pool.tile([P, 512], F32, name="mm")
+                bank = tp_pool.tile([P, 512], F32, name="bank")
                 tiles["xw", g, half] = bank
                 for s in range(2):
                     rows = slice(128 * (2 * half + s), 128 * (2 * half + s) + 128)
                     nc.tensor.matmul_mx(out=bank[:, H * s : H * s + H], lhsT=h_cod[g][:, rows].bitcast(FP8X4), lhsT_scale=h_scl[g][:, rows], rhs=w_cod[:].bitcast(FP8X4), rhs_scale=w_scl[:], start=True, stop=True)
                 return
             cols = slice(128 * half, 128 * half + 128)
-            bank = mm_pool.tile([P, 512], F32, name="mm")
+            bank = tp_pool.tile([P, 512], F32, name="bank")
             tiles["xw", g, half] = bank
             for s in range(4):
                 rows = slice(128 * s, 128 * s + 128)
@@ -232,7 +225,7 @@ def tile_gcnclassifer_pa_kernel(tc, h_enc, adj, w_bytes, w_scale, b, out):
             nc.tensor.matmul_mx(out=tiles["ag", r][:, 0:H], lhsT=a_cod[r][:, rows].bitcast(FP8X4), lhsT_scale=a_scl[r][:, rows], rhs=y_cod[c][:].bitcast(FP8X4), rhs_scale=y_scl[c][:], start=(c == 0), stop=(c == 3))
 
         def do_aga(r):
-            tiles["ag", r] = mm_pool.tile([P, 512], F32, name="mm")
+            tiles["ag", r] = tp_pool.tile([P, 512], F32, name="bank")
             for c in range(3):
                 mx_pass(r, c)
 
@@ -262,7 +255,7 @@ def tile_gcnclassifer_pa_kernel(tc, h_enc, adj, w_bytes, w_scale, b, out):
             nc.vector.quantize_mx(out=w_cod[:].bitcast(FP8X4), scales=w_scl[:], in_=w_grp[:].rearrange("p n t -> p (n t)"))
 
         def do_biasm():
-            tiles["bias"] = mm_pool.tile([P, 512], F32, name="mm")
+            tiles["bias"] = tp_pool.tile([P, 512], F32, name="bank")
             nc.tensor.matmul(tiles["bias"][:, 0:H], lhsT=ones[:], rhs=b_row[:], start=True, stop=True)
 
         def do_biasc():
@@ -276,12 +269,9 @@ def tile_gcnclassifer_pa_kernel(tc, h_enc, adj, w_bytes, w_scale, b, out):
             nc.scalar.activation(res[:, H * i : H * i + H], tiles["sums", r // 2][:, H * i : H * i + H], ACT.Relu)
             nc.sync.dma_start(out=o_view[r // 4][:, r % 4, :], in_=res[:, H * i : H * i + H])
 
-        table = {"wact": do_wact, "wcp": do_wcp, "wq": do_wq, "deg": do_deg, "pm": do_pm, "pow": do_pow, "tr": do_tr, "cp": do_cp, "q": do_q, "htr": do_htr, "hcp": do_hcp, "hq": do_hq, "xw": do_xw, "yt": do_yt, "yq": do_yq, "ys": do_ys, "yi": do_yi, "gg": do_gg, "dega": do_dega, "biasm": do_biasm, "biasc": do_biasc, "rs": do_rs, "aga": do_aga, "ag": do_ag, "st": do_st, "rl": do_rl, "n1": do_n1}
+        table = {"wact": do_wact, "wcp": do_wcp, "wq": do_wq, "deg": do_deg, "pm": do_pm, "pow": do_pow, "tr": do_tr, "cp": do_cp, "q": do_q, "htr": do_htr, "hcp": do_hcp, "hq": do_hq, "xw": do_xw, "yt": do_yt, "yq": do_yq, "ys": do_ys, "yi": do_yi, "gg": do_gg, "dega": do_dega, "biasm": do_biasm, "biasc": do_biasc, "rs": do_rs, "aga": do_aga, "ag": do_ag, "st": do_st, "rl": do_rl}
         for token in ORDER:
-            word = token if token.startswith("n1") else token.replace(".", " ")
-            if token.startswith("n1"):
-                do_n1(int(token[2:]))
-                continue
+            word = token.replace(".", " ")
             names = [n for n in table if word.startswith(n) and all(ch in "0123456789 " for ch in word[len(n) :])]
             n = names[0]
             table[n](*[int(v) for v in word[len(n) :].split(" ") if v])

@@ -16,262 +16,298 @@ ALU = mybir.AluOpType
 ACT = mybir.ActivationFunctionType
 
 P = 128
-GROUPS = 4
-TILES = 16
-KIND = "V V V V V G V V S G P V G V V P".split(" ")
-YK = "VVVV"
-LOADS = "a0 b0 w a1 a2 a3 a4 a5 h0 a6 h1 a7 a8 a9 h2 a10 a11 a12 h3 a13 a14 a15".split(" ")
-ORDER = "dega0 wact deg0 tr0.0 tr0.1 deg1 cp0.0 wcp deg2 tr1.0 tr1.1 cp0.1 deg3 tr2.0 cp1.0 tr2.1 cp1.1 q0 tr3.0 pow0 wq cp2.0 tr3.1 deg4 gg5 tr5.0 cp2.1 tr5.1 cp3.0 q1 htr0.0 cp3.1 htr0.1 q2 hcp0.0 tr4.0 deg6 hcp0.1 tr4.1 cp4.0 htr1.0 hq0 cp4.1 htr1.1 q3 hcp1.0 tr6.0 deg7 tr6.1 hcp1.1 xw0.0 cp5.0 xw0.1 yt0.0 cp5.1 biasm tr7.0 yt0.1 cp6.0 tr7.1 gg9 hq1 biasc tr9.0 cp6.1 yq0 tr9.1 deg5 cp7.0 q4 htr2.0 pow1 cp7.1 q5 htr2.1 hcp2.0 pm10 q6 hcp2.1 q7 cp9.0 deg11 tr10.0 cp9.1 tr10.1 cp10.0 tr12.0 hq2 cp10.1 htr3.0 deg10 q9 cp12.0 htr3.1 q10 hcp3.0 tr11.0 tr11.1 deg13 hcp3.1 gg12 tr12.1 cp11.0 xw1.0 hq3 cp11.1 xw1.1 xw2.0 yt1.0 cp12.1 xw2.1 xw3.0 yt1.1 deg8 xw3.1 pm15 deg9 deg14 tr13.0 yq1 tr13.1 deg15 q11 pow2 tr8.0 cp13.0 tr8.1 yt2.0 cp8.0 tr14.0 yt2.1 cp8.1 tr14.1 q12 tr15.0 cp13.1 yq2 tr15.1 cp14.0 deg12 q8 aga0 pow3 cp14.1 q13 aga1 cp15.0 aga2 yt3.0 aga3 cp15.1 yt3.1 aga4 aga5 q14 aga6 yq3 aga7 q15 ag0 ag1 ag2 st0 ag3 ag4 ag5 st1 ag6 ag7 st2 aga8 rl1 st3 aga9 st4 ag8 rl3 st5 aga10 st6 ag9 aga11 rl5 st7 st8 ag10 aga12 rl7 st9 ag11 st10 aga13 rl9 st11 ag12 aga14 st12 rl11 ag13 aga15 st13 ag14 ag15 st14 rl13 st15 rs14 rs15".split(" ")
+PACK = 4
+PASS = P * PACK
+GROUPS = N // PASS
+TILES = N // P
+
+DEGREE = "VVVVVTVVVSVVVTTV"
+
+LOADS = """
+half:0 half:1 w:0 adj:1 adj:2 bias:0 adj:3 adj:4 adj:5 adj:6 h:0 h:1 adj:7 h:2 adj:8 adj:9 h:3 adj:10 adj:11 adj:12
+adj:13 adj:14 adj:15
+"""
+
+ORDER = """
+degree_half:0 w_widen degree_half:1 turn:0:0 turn:0:1 degree:1 copy:0:0 w_group degree:2 turn:1:0 turn:1:1 copy:0:1
+degree:3 turn:2:0 copy:1:0 turn:2:1 copy:1:1 quantise:0 turn:3:0 root:0 w_quantise copy:2:0 turn:3:1 degree:4
+partial:5 copy:2:1 copy:3:0 degree:6 copy:3:1 turn:4:0 turn:4:1 degree:5 copy:4:0 h_turn:0:0 quantise:1 copy:4:1
+h_turn:0:1 quantise:2 h_copy:0:0 h_turn:1:0 quantise:3 h_copy:0:1 h_turn:1:1 quantise:4 h_copy:1:0 turn:5:0 degree:7
+turn:5:1 h_copy:1:1 h_turn:2:0 copy:5:0 h_quantise:0 h_turn:2:1 copy:5:1 h_quantise:1 turn:6:0 h_copy:2:0 turn:6:1
+degree:8 h_copy:2:1 turn:7:0 turn:7:1 root:1 copy:6:0 project:0:0 h_quantise:2 copy:6:1 project:0:1 quantise:5
+project:1:0 copy:7:0 project:1:1 scale_y:0:0 project:2:0 copy:7:1 scale_y:0:1 project:2:1 degree:9 bias_spread
+scale_y:1:0 h_turn:3:0 y_quantise:0 h_turn:3:1 scale_y:1:1 turn:8:0 degree:10 turn:8:1 bias_copy turn:9:0 h_copy:3:0
+turn:9:1 y_quantise:1 h_copy:3:1 degree:11 partial:13 copy:8:0 copy:8:1 h_quantise:3 partial:14 root:2 copy:9:0
+degree:12 copy:9:1 degree:13 turn:10:0 scale_y:2:0 degree:14 turn:10:1 scale_y:2:1 copy:10:0 turn:11:0 turn:11:1
+degree:15 copy:10:1 turn:12:0 copy:11:0 turn:12:1 y_quantise:2 copy:11:1 turn:13:0 quantise:6 turn:13:1 root:3
+copy:12:0 quantise:7 turn:14:0 copy:12:1 quantise:8 turn:14:1 copy:13:0 quantise:9 turn:15:0 copy:13:1 turn:15:1
+quantise:10 project:3:0 copy:14:0 quantise:11 project:3:1 copy:14:1 scale_y:3:0 aggregate:0 copy:15:0 aggregate:1
+scale_y:3:1 copy:15:1 aggregate:2 quantise:12 aggregate:3 y_quantise:3 aggregate:4 quantise:13 aggregate:5 quantise:14
+aggregate_last:0 aggregate_last:1 aggregate_last:2 aggregate_last:3 scale_sum:0 aggregate_last:4 aggregate_last:5
+scale_sum:1 aggregate:6 scale_sum:2 aggregate:7 finish_pair:1 scale_sum:3 aggregate_last:6 scale_sum:4 aggregate:8
+finish_pair:3 scale_sum:5 aggregate_last:7 scale_sum:6 aggregate:9 finish_pair:5 scale_sum:7 aggregate_last:8
+aggregate:10 quantise:15 finish_pair:7 aggregate_last:9 aggregate:11 scale_sum:8 scale_sum:9 aggregate_last:10
+aggregate:12 scale_sum:10 finish_pair:9 aggregate_last:11 aggregate:13 scale_sum:11 aggregate_last:12 aggregate:14
+scale_sum:12 finish_pair:11 aggregate_last:13 aggregate:15 scale_sum:13 aggregate_last:14 aggregate_last:15
+scale_sum:14 finish_pair:13 scale_sum:15 finish_one:14 finish_one:15
+"""
 
 
-def tile_gcnclassifer_pa_kernel(tc, h_enc, adj, w_bytes, w_scale, b, out):
+def tile_gcnclassifer_pa_kernel(tc, h_enc, adj, w_bytes, w_scale, bias, out):
     nc = tc.nc
-    h_view = h_enc.rearrange("(g p s) e -> g p s e", p=P, s=4)
-    a_view = adj.rearrange("(g p s) j -> g s p j", p=P, s=4)
-    o_view = out.rearrange("(g p s) h -> g p s h", p=P, s=4)
+    h_view = h_enc.rearrange("(g p s) e -> g p s e", p=P, s=PACK)
+    adj_view = adj.rearrange("(g p s) j -> g s p j", p=P, s=PACK)
+    out_view = out.rearrange("(g p s) n -> g p s n", p=P, s=PACK)
 
     with ExitStack() as ctx:
         keep = ctx.enter_context(tc.tile_pool(name="keep", bufs=1))
         work = ctx.enter_context(tc.tile_pool(name="work", bufs=2))
-        ordered = ctx.enter_context(tc.tile_pool(name="ordered", bufs=10))
+        reordered = ctx.enter_context(tc.tile_pool(name="reordered", bufs=8))
         tail = ctx.enter_context(tc.tile_pool(name="tail", bufs=4))
-        tp_pool = ctx.enter_context(tc.psum_pool(name="tp", bufs=8))
+        banks = ctx.enter_context(tc.psum_pool(name="banks", bufs=8))
         ctx.enter_context(tc.manual_schedule())
 
-        a_raw = [keep.tile([P, N], BF16, name=f"a_raw{r}", align_bytes=64) for r in range(TILES)]
-        h_raw = [keep.tile([P, 4 * E], BF16, name=f"h_raw{g}", align_bytes=64) for g in range(GROUPS)]
-        a_ord = {}
-        a_cod = [keep.tile([P, N // 4], U32, name=f"a_cod{r}", align_bytes=64) for r in range(TILES)]
-        a_scl = [keep.tile([P, N // 4], U8, name=f"a_scl{r}", align_bytes=64) for r in range(TILES)]
-        h_cod = [keep.tile([P, 512], U32, name=f"h_cod{g}", align_bytes=64) for g in range(GROUPS)]
-        h_scl = [keep.tile([P, 512], U8, name=f"h_scl{g}", align_bytes=64) for g in range(GROUPS)]
-        y_cod = [keep.tile([P, H], U32, name=f"y_cod{g}", align_bytes=64) for g in range(GROUPS)]
-        y_scl = [keep.tile([P, H], U8, name=f"y_scl{g}", align_bytes=64) for g in range(GROUPS)]
-        w_cod = keep.tile([P, H], U32, name="w_cod", align_bytes=64)
-        w_scl = keep.tile([P, H], U8, name="w_scl", align_bytes=64)
-        w_raw = keep.tile([P, 4 * H], U8, name="w_raw", align_bytes=64)
-        w_sc = keep.tile([P, 4], F32, name="w_sc")
-        w_pl = keep.tile([P, 4, H], BF16, name="w_pl", align_bytes=64)
-        w_grp = keep.tile([P, H, 4], BF16, name="w_grp", align_bytes=64)
-        ident = keep.tile([P, P], F32, name="ident")
-        ident_b = keep.tile([P, P], BF16, name="ident_b")
+        adj_raw = [keep.tile([P, N], BF16, name=f"adj_raw{r}", align_bytes=64) for r in range(TILES)]
+        adj_codes = [keep.tile([P, PASS], U32, name=f"adj_codes{r}", align_bytes=64) for r in range(TILES)]
+        adj_scales = [keep.tile([P, PASS], U8, name=f"adj_scales{r}", align_bytes=64) for r in range(TILES)]
+        h_raw = [keep.tile([P, PACK * E], BF16, name=f"h_raw{g}", align_bytes=64) for g in range(GROUPS)]
+        h_codes = [keep.tile([P, PASS], U32, name=f"h_codes{g}", align_bytes=64) for g in range(GROUPS)]
+        h_scales = [keep.tile([P, PASS], U8, name=f"h_scales{g}", align_bytes=64) for g in range(GROUPS)]
+        y_codes = [keep.tile([P, H], U32, name=f"y_codes{g}", align_bytes=64) for g in range(GROUPS)]
+        y_scales = [keep.tile([P, H], U8, name=f"y_scales{g}", align_bytes=64) for g in range(GROUPS)]
+        w_raw = keep.tile([P, PACK * H], U8, name="w_raw", align_bytes=64)
+        w_factor = keep.tile([P, PACK], F32, name="w_factor")
+        w_wide = keep.tile([P, PACK, H], BF16, name="w_wide", align_bytes=64)
+        w_grouped = keep.tile([P, H, PACK], BF16, name="w_grouped", align_bytes=64)
+        w_codes = keep.tile([P, H], U32, name="w_codes", align_bytes=64)
+        w_scales = keep.tile([P, H], U8, name="w_scales", align_bytes=64)
+        identity = keep.tile([P, P], F32, name="identity")
+        identity_bf16 = keep.tile([P, P], BF16, name="identity_bf16")
         ones = keep.tile([P, P], BF16, name="ones")
-        b_row = keep.tile([P, H], BF16, name="b_row")
-        b_all = keep.tile([P, H], F32, name="b_all")
-        deg = keep.tile([P, TILES], F32, name="deg")
+        bias_row = keep.tile([P, H], BF16, name="bias_row")
+        bias_all = keep.tile([P, H], F32, name="bias_all")
+        degree = keep.tile([P, TILES], F32, name="degree")
         dis = keep.tile([P, TILES], F32, name="dis")
-        part_deg = keep.tile([P, 1], F32, name="part_deg")
-        warm = keep.tile([P, 1], F32, name="warm")
+        half_degree = keep.tile([P, 1], F32, name="half_degree")
+        unused = keep.tile([P, P], F32, name="unused")
+        table_load = keep.tile([P, 1], F32, name="table_load")
 
-        def load_a(r):
-            nc.sync.dma_start(out=a_raw[r][:], in_=a_view[r // 4, r % 4])
-
-        def load_h(g):
-            nc.sync.dma_start(out=h_raw[g][:].rearrange("p (s e) -> p s e", s=4), in_=h_view[g])
-
-        nc.vector.memset(b_row[:], 0.0)
-        for item in LOADS:
-            if item == "a3":
-                nc.sync.dma_start(out=b_row[0:1, :], in_=b.rearrange("(o n) -> o n", o=1))
-            if item in ("a0", "b0"):
-                half = slice(0, 1024) if item == "a0" else slice(1024, 2048)
-                nc.sync.dma_start(out=a_raw[0][:, half], in_=a_view[0, 0][:, half])
-            elif item == "w":
-                nc.sync.dma_start(out=w_raw[:].rearrange("p (t n) -> p t n", t=4), in_=w_bytes.rearrange("(p t) n -> p t n", t=4))
-                nc.sync.dma_start(out=w_sc[:], in_=w_scale.rearrange("(p t) o -> p (t o)", t=4))
-            elif item[0] == "p":
-                load_a(int(item[1:]))
-                load_a(int(item[1:]) + 1)
-            elif item[0] == "a":
-                load_a(int(item[1:]))
+        nc.vector.memset(bias_row[:], 0.0)
+        for load in LOADS.split():
+            name, index = load.split(":")
+            if name == "w":
+                nc.sync.dma_start(out=w_raw[:].rearrange("p (t n) -> p t n", t=PACK), in_=w_bytes.rearrange("(p t) n -> p t n", t=PACK))
+                nc.sync.dma_start(out=w_factor[:], in_=w_scale.rearrange("(p t) o -> p (t o)", t=PACK))
+            elif name == "bias":
+                nc.sync.dma_start(out=bias_row[0:1, :], in_=bias.rearrange("(o n) -> o n", o=1))
+            elif name == "half":
+                cols = slice(N // 2 * int(index), N // 2 * (int(index) + 1))
+                nc.sync.dma_start(out=adj_raw[0][:, cols], in_=adj_view[0, 0][:, cols])
+            elif name == "adj":
+                nc.sync.dma_start(out=adj_raw[int(index)][:], in_=adj_view[int(index) // PACK, int(index) % PACK])
             else:
-                load_h(int(item[1:]))
+                nc.sync.dma_start(out=h_raw[int(index)][:].rearrange("p (s e) -> p s e", s=PACK), in_=h_view[int(index)])
 
-        nc.vector.memset(warm[:], 1.0)
-        make_identity(nc, ident[:])
+        nc.vector.memset(table_load[:], 1.0)
+        make_identity(nc, identity[:])
         nc.vector.memset(ones[:], 1.0)
-        if any(k == "P" for k in KIND):
-            make_identity(nc, ident_b[:])
-        nc.scalar.activation(warm[:], warm[:], ACT.Abs_reciprocal_sqrt)
+        make_identity(nc, identity_bf16[:])
+        nc.scalar.activation(table_load[:], table_load[:], ACT.Abs_reciprocal_sqrt)
 
-        tiles = {}
+        held = {}
 
-        def half_degree(half, start, col):
-            src = a_raw[0][:, 1024 * half : 1024 * half + 1024].rearrange("p (n u e) -> p u n e", u=2, e=2)
-            dst = a_ord[0][:].rearrange("p (u n e) -> p u n e", u=2, e=2)[:, :, 256 * half : 256 * half + 256, :]
-            nc.vector.tensor_scalar(out=dst, in0=src, scalar1=1.0, scalar2=start, op0=ALU.mult, op1=ALU.add, accum_out=col)
+        def word_order(tile, low, high):
+            return tile[:, PACK * low : PACK * high].rearrange("p (n u e) -> p u n e", u=2, e=2)
 
-        def do_dega(r):
-            a_ord[0] = ordered.tile([P, N], BF16, name="a_ord", align_bytes=64)
-            half_degree(0, None, part_deg[:])
+        def by_u(tile, low, high):
+            return tile[:].rearrange("p (u n e) -> p u n e", u=2, e=2)[:, :, low:high, :]
 
-        def do_deg(r):
-            col = deg[:, r : r + 1]
-            if KIND[r] == "G":
-                nc.vector.tensor_reduce(out=col, in_=tiles["gg", r][:, 0:64], axis=mybir.AxisListType.X, op=ALU.add)
+        def degree_half(half):
+            if half == 0:
+                held["reordered", 0] = reordered.tile([P, N], BF16, name="adj_reordered", align_bytes=64)
+            low, high = N // 8 * half, N // 8 * (half + 1)
+            nc.vector.tensor_scalar(
+                out=by_u(held["reordered", 0], low, high),
+                in0=word_order(adj_raw[0], low, high),
+                scalar1=1.0,
+                scalar2=half_degree[:] if half else None,
+                op0=ALU.mult,
+                op1=ALU.add,
+                accum_out=degree[:, 0:1] if half else half_degree[:],
+            )
+
+        def degree_of(r):
+            col = degree[:, r : r + 1]
+            if DEGREE[r] == "T":
+                nc.scalar.activation(unused[:], held["partial", r][:, 0:P], ACT.Copy, accum_out=col)
                 return
-            if KIND[r] == "P":
-                nc.vector.tensor_reduce(out=col, in_=tiles["pm", r][:, 0:P], axis=mybir.AxisListType.X, op=ALU.add)
-                return
-            if r == 0:
-                half_degree(1, part_deg[:], col)
-                return
-            src = a_raw[r][:].rearrange("p (n u e) -> p u n e", u=2, e=2)
-            a_ord[r] = ordered.tile([P, N], BF16, name="a_ord", align_bytes=64)
-            dst = a_ord[r][:].rearrange("p (u n e) -> p u n e", u=2, e=2)
-            if KIND[r] == "S":
+            held["reordered", r] = reordered.tile([P, N], BF16, name="adj_reordered", align_bytes=64)
+            src = word_order(adj_raw[r], 0, N // PACK)
+            dst = by_u(held["reordered", r], 0, N // PACK)
+            if DEGREE[r] == "S":
                 nc.scalar.activation(dst, src, ACT.Copy, accum_out=col)
             else:
                 nc.vector.tensor_scalar(out=dst, in0=src, scalar1=1.0, scalar2=None, op0=ALU.mult, op1=ALU.add, accum_out=col)
 
-        def do_gg(r):
-            part = work.tile([P, 1024], F32, name="part", align_bytes=64)
-            tiles["gg", r] = part
-            for c in range(4):
-                cols = slice(256 * c, 256 * c + 256)
-                nc.gpsimd.tensor_tensor(out=part[:, cols], in0=a_raw[r][:, cols], in1=a_raw[r][:, 1024 + 256 * c : 1280 + 256 * c], op=ALU.add)
-            width = 512
-            while width >= 64:
-                for lo in range(0, width, 256):
-                    hi = min(width, lo + 256)
-                    nc.gpsimd.tensor_tensor(out=part[:, lo:hi], in0=part[:, lo:hi], in1=part[:, width + lo : width + hi], op=ALU.add)
-                width = width // 2
+        def partial(r):
+            bank = banks.tile([P, PASS], F32, name="bank")
+            held["partial", r] = bank
+            blocks = N // P
+            for b in range(blocks):
+                nc.tensor.matmul(bank[:, 0:P], lhsT=identity_bf16[:], rhs=adj_raw[r][:, P * b : P * b + P], start=(b == 0), stop=(b == blocks - 1))
 
-        def do_pm(r):
-            bank = tp_pool.tile([P, 512], F32, name="bank")
-            tiles["pm", r] = bank
-            for c in range(16):
-                nc.tensor.matmul(bank[:, 0:P], lhsT=ident_b[:], rhs=a_raw[r][:, P * c : P * c + P], start=(c == 0), stop=(c == 15))
+        def inverse_root(g):
+            cols = slice(PACK * g, PACK * g + PACK)
+            nc.scalar.activation(dis[:, cols], degree[:, cols], ACT.Abs_reciprocal_sqrt)
 
-        def do_pow(g):
-            cols = slice(4 * g, 4 * g + 4)
-            nc.scalar.activation(dis[:, cols], deg[:, cols], ACT.Abs_reciprocal_sqrt)
-
-        def do_tr(r, half):
-            bank = tp_pool.tile([P, 512], F32, name="bank")
-            tiles["tp", r, half] = bank
-            raw = KIND[r][0] in "NPG"
-            words = a_raw[r][:].bitcast(F32) if raw else a_ord[r][:].bitcast(F32)
-            for c2 in range(2):
+        def turn(r, half):
+            bank = banks.tile([P, PASS], F32, name="bank")
+            held["turned", r, half] = bank
+            for i in range(2):
+                c = 2 * half + i
                 for u in range(2):
-                    c = 2 * half + c2
-                    src = words[:, 256 * c + u : 256 * c + 256 : 2] if raw else words[:, 512 * u + 128 * c : 512 * u + 128 * c + 128]
-                    nc.tensor.transpose(bank[:, 256 * c2 + 128 * u : 256 * c2 + 128 * u + 128], src, ident[:])
+                    if DEGREE[r] == "T":
+                        words = adj_raw[r][:].bitcast(F32)[:, 2 * P * c + u : 2 * P * (c + 1) : 2]
+                    else:
+                        words = held["reordered", r][:].bitcast(F32)[:, N // 4 * u + P * c : N // 4 * u + P * (c + 1)]
+                    nc.tensor.transpose(bank[:, P * (2 * i + u) : P * (2 * i + u + 1)], words, identity[:])
 
-        def do_cp(r, half):
-            if ("a_grp", r) not in tiles:
-                if KIND[r] in "VS":
-                    tiles["a_grp", r] = a_raw[r]
-                else:
-                    tiles["a_grp", r] = work.tile([P, N], BF16, name="a_grp", align_bytes=64)
-            nc.scalar.copy(out=tiles["a_grp", r][:].bitcast(F32)[:, 512 * half : 512 * half + 512].rearrange("p (c i u) -> p c i u", c=2, u=2), in_=tiles["tp", r, half][:].rearrange("p (c u i) -> p c i u", c=2, u=2))
+        def copy_turned(r, half):
+            if ("grouped", r) not in held:
+                held["grouped", r] = work.tile([P, N], BF16, name="adj_grouped", align_bytes=64) if DEGREE[r] == "T" else adj_raw[r]
+            nc.scalar.copy(
+                out=held["grouped", r][:].bitcast(F32)[:, PASS * half : PASS * (half + 1)].rearrange("p (c i u) -> p c i u", c=2, u=2),
+                in_=held["turned", r, half][:].rearrange("p (c u i) -> p c i u", c=2, u=2),
+            )
 
-        def do_q(r):
-            nc.vector.quantize_mx(out=a_cod[r][:].bitcast(FP8X4), scales=a_scl[r][:], in_=tiles["a_grp", r][:])
+        def quantise(r):
+            nc.vector.quantize_mx(out=adj_codes[r][:].bitcast(FP8X4), scales=adj_scales[r][:], in_=held["grouped", r][:])
 
-        def do_htr(g, half):
-            bank = tp_pool.tile([P, 512], F32, name="bank")
-            tiles["htp", g, half] = bank
+        def h_turn(g, half):
+            bank = banks.tile([P, PASS], F32, name="bank")
+            held["h_turned", g, half] = bank
             words = h_raw[g][:].bitcast(F32)
-            for s2 in range(2):
+            for i in range(2):
+                s = 2 * half + i
                 for u in range(2):
-                    s = 2 * half + s2
-                    nc.tensor.transpose(bank[:, 256 * s2 + 128 * u : 256 * s2 + 128 * u + 128], words[:, 256 * s + u : 256 * s + 256 : 2], ident[:])
+                    nc.tensor.transpose(bank[:, P * (2 * i + u) : P * (2 * i + u + 1)], words[:, 2 * P * s + u : 2 * P * (s + 1) : 2], identity[:])
 
-        def do_hcp(g, half):
-            if ("h_grp", g) not in tiles:
-                tiles["h_grp", g] = work.tile([P, 4 * E], BF16, name="h_grp", align_bytes=64)
-            nc.scalar.copy(out=tiles["h_grp", g][:].bitcast(F32)[:, 512 * half : 512 * half + 512].rearrange("p (s j u) -> p s j u", s=2, u=2), in_=tiles["htp", g, half][:].rearrange("p (s u j) -> p s j u", s=2, u=2))
+        def h_copy(g, half):
+            if ("h_grouped", g) not in held:
+                held["h_grouped", g] = work.tile([P, PACK * E], BF16, name="h_grouped", align_bytes=64)
+            nc.scalar.copy(
+                out=held["h_grouped", g][:].bitcast(F32)[:, PASS * half : PASS * (half + 1)].rearrange("p (s i u) -> p s i u", s=2, u=2),
+                in_=held["h_turned", g, half][:].rearrange("p (s u i) -> p s i u", s=2, u=2),
+            )
 
-        def do_hq(g):
-            nc.vector.quantize_mx(out=h_cod[g][:].bitcast(FP8X4), scales=h_scl[g][:], in_=tiles["h_grp", g][:])
+        def h_quantise(g):
+            nc.vector.quantize_mx(out=h_codes[g][:].bitcast(FP8X4), scales=h_scales[g][:], in_=held["h_grouped", g][:])
 
-        def do_xw(g, half):
-            if YK[g] == "S":
-                bank = tp_pool.tile([P, 512], F32, name="bank")
-                tiles["xw", g, half] = bank
-                for s in range(2):
-                    rows = slice(128 * (2 * half + s), 128 * (2 * half + s) + 128)
-                    nc.tensor.matmul_mx(out=bank[:, H * s : H * s + H], lhsT=h_cod[g][:, rows].bitcast(FP8X4), lhsT_scale=h_scl[g][:, rows], rhs=w_cod[:].bitcast(FP8X4), rhs_scale=w_scl[:], start=True, stop=True)
-                return
-            cols = slice(128 * half, 128 * half + 128)
-            bank = tp_pool.tile([P, 512], F32, name="bank")
-            tiles["xw", g, half] = bank
-            for s in range(4):
-                rows = slice(128 * s, 128 * s + 128)
-                nc.tensor.matmul_mx(out=bank[:, rows], lhsT=h_cod[g][:, rows].bitcast(FP8X4), lhsT_scale=h_scl[g][:, rows], rhs=w_cod[:, cols].bitcast(FP8X4), rhs_scale=w_scl[:, cols], start=True, stop=True)
+        def w_widen():
+            for t in range(PACK):
+                nc.scalar.activation(w_wide[:, t, :], w_raw[:, H * t : H * (t + 1)].bitcast(FP8), ACT.Copy, scale=w_factor[:, t : t + 1])
 
-        def do_yt(g, half):
-            if ("y_grp", g) not in tiles:
-                tiles["y_grp", g] = work.tile([P, 4 * H], BF16, name="y_grp", align_bytes=64)
-            nc.vector.tensor_tensor(out=tiles["y_grp", g][:, 512 * half : 512 * half + 512].rearrange("p (n s) -> p n s", s=4), in0=tiles["xw", g, half][:].rearrange("p (s n) -> p n s", s=4), in1=dis[:, 4 * g : 4 * g + 4].unsqueeze(1).to_broadcast([P, 128, 4]), op=ALU.mult)
+        def w_group():
+            nc.scalar.copy(out=w_grouped[:], in_=w_wide[:].rearrange("p t n -> p n t"))
 
-        def do_ys(g, half):
-            if ("y_pl", g) not in tiles:
-                tiles["y_pl", g] = work.tile([P, 4 * H], BF16, name="y_pl", align_bytes=64)
-            for s in range(2):
-                col = 2 * half + s
-                nc.scalar.activation(tiles["y_pl", g][:, H * col : H * col + H], tiles["xw", g, half][:, H * s : H * s + H], ACT.Copy, scale=dis[:, 4 * g + col : 4 * g + col + 1])
+        def w_quantise():
+            nc.vector.quantize_mx(out=w_codes[:].bitcast(FP8X4), scales=w_scales[:], in_=w_grouped[:].rearrange("p n t -> p (n t)"))
 
-        def do_yi(g):
-            tiles["y_grp", g] = work.tile([P, 4 * H], BF16, name="y_grp", align_bytes=64)
-            nc.gpsimd.tensor_scalar(out=tiles["y_grp", g][:].rearrange("p (n s) -> p n s", s=4), in0=tiles["y_pl", g][:].rearrange("p (s n) -> p n s", s=4), scalar1=1.0, scalar2=0.0, op0=ALU.mult, op1=ALU.add)
+        def project(g, half):
+            cols = slice(P * half, P * (half + 1))
+            bank = banks.tile([P, PASS], F32, name="bank")
+            held["xw", g, half] = bank
+            for s in range(PACK):
+                rows = slice(P * s, P * (s + 1))
+                nc.tensor.matmul_mx(
+                    out=bank[:, rows],
+                    lhsT=h_codes[g][:, rows].bitcast(FP8X4),
+                    lhsT_scale=h_scales[g][:, rows],
+                    rhs=w_codes[:, cols].bitcast(FP8X4),
+                    rhs_scale=w_scales[:, cols],
+                    start=True,
+                    stop=True,
+                )
 
-        def do_yq(g):
-            nc.vector.quantize_mx(out=y_cod[g][:].bitcast(FP8X4), scales=y_scl[g][:], in_=tiles["y_grp", g][:])
+        def scale_y(g, half):
+            if ("y", g) not in held:
+                held["y", g] = work.tile([P, PACK * H], BF16, name="y_grouped", align_bytes=64)
+            nc.vector.tensor_tensor(
+                out=held["y", g][:, PASS * half : PASS * (half + 1)].rearrange("p (n s) -> p n s", s=PACK),
+                in0=held["xw", g, half][:].rearrange("p (s n) -> p n s", s=PACK),
+                in1=dis[:, PACK * g : PACK * (g + 1)].unsqueeze(1).to_broadcast([P, P, PACK]),
+                op=ALU.mult,
+            )
 
-        def mx_pass(r, c):
-            rows = slice(128 * c, 128 * c + 128)
-            nc.tensor.matmul_mx(out=tiles["ag", r][:, 0:H], lhsT=a_cod[r][:, rows].bitcast(FP8X4), lhsT_scale=a_scl[r][:, rows], rhs=y_cod[c][:].bitcast(FP8X4), rhs_scale=y_scl[c][:], start=(c == 0), stop=(c == 3))
+        def y_quantise(g):
+            nc.vector.quantize_mx(out=y_codes[g][:].bitcast(FP8X4), scales=y_scales[g][:], in_=held["y", g][:])
 
-        def do_aga(r):
-            tiles["ag", r] = tp_pool.tile([P, 512], F32, name="bank")
-            for c in range(3):
-                mx_pass(r, c)
+        def aggregate_pass(r, c):
+            rows = slice(P * c, P * (c + 1))
+            nc.tensor.matmul_mx(
+                out=held["sum", r][:, 0:H],
+                lhsT=adj_codes[r][:, rows].bitcast(FP8X4),
+                lhsT_scale=adj_scales[r][:, rows],
+                rhs=y_codes[c][:].bitcast(FP8X4),
+                rhs_scale=y_scales[c][:],
+                start=(c == 0),
+                stop=(c == GROUPS - 1),
+            )
 
-        def do_ag(r):
-            mx_pass(r, 3)
+        def aggregate(r):
+            held["sum", r] = banks.tile([P, PASS], F32, name="bank")
+            for c in range(GROUPS - 1):
+                aggregate_pass(r, c)
 
-        def do_st(r):
+        def aggregate_last(r):
+            aggregate_pass(r, GROUPS - 1)
+
+        def bias_spread():
+            held["bias", 0] = banks.tile([P, PASS], F32, name="bank")
+            nc.tensor.matmul(held["bias", 0][:, 0:H], lhsT=ones[:], rhs=bias_row[:], start=True, stop=True)
+
+        def bias_copy():
+            nc.scalar.copy(out=bias_all[:], in_=held["bias", 0][:, 0:H])
+
+        def scale_sum(r):
             i = r % 2
-            if ("sums", r // 2) not in tiles:
-                tiles["sums", r // 2] = tail.tile([P, 2 * H], F32, name="sums")
-            nc.vector.scalar_tensor_tensor(out=tiles["sums", r // 2][:, H * i : H * i + H], in0=tiles["ag", r][:, 0:H], scalar=dis[:, r : r + 1], in1=b_all[:], op0=ALU.mult, op1=ALU.add)
+            if ("scaled", r // 2) not in held:
+                held["scaled", r // 2] = tail.tile([P, 2 * H], F32, name="scaled")
+            nc.vector.scalar_tensor_tensor(
+                out=held["scaled", r // 2][:, H * i : H * (i + 1)],
+                in0=held["sum", r][:, 0:H],
+                scalar=dis[:, r : r + 1],
+                in1=bias_all[:],
+                op0=ALU.mult,
+                op1=ALU.add,
+            )
 
-        def do_rl(r):
+        def finish_pair(r):
             pair = r // 2
-            res = tail.tile([P, 2 * H], F32, name="res")
-            nc.scalar.activation(res[:], tiles["sums", pair][:], ACT.Relu)
-            nc.sync.dma_start(out=o_view[pair // 2][:, 2 * (pair % 2) : 2 * (pair % 2) + 2, :], in_=res[:].rearrange("p (s n) -> p s n", s=2))
+            result = tail.tile([P, 2 * H], F32, name="result")
+            nc.scalar.activation(result[:], held["scaled", pair][:], ACT.Relu)
+            s = 2 * (pair % 2)
+            nc.sync.dma_start(out=out_view[pair // 2][:, s : s + 2, :], in_=result[:].rearrange("p (s n) -> p s n", s=2))
 
-        def do_wact():
-            for t in range(4):
-                nc.scalar.activation(w_pl[:, t, :], w_raw[:, H * t : H * t + H].bitcast(FP8), ACT.Copy, scale=w_sc[:, t : t + 1])
-
-        def do_wcp():
-            nc.scalar.copy(out=w_grp[:], in_=w_pl[:].rearrange("p t n -> p n t"))
-
-        def do_wq():
-            nc.vector.quantize_mx(out=w_cod[:].bitcast(FP8X4), scales=w_scl[:], in_=w_grp[:].rearrange("p n t -> p (n t)"))
-
-        def do_biasm():
-            tiles["bias"] = tp_pool.tile([P, 512], F32, name="bank")
-            nc.tensor.matmul(tiles["bias"][:, 0:H], lhsT=ones[:], rhs=b_row[:], start=True, stop=True)
-
-        def do_biasc():
-            nc.scalar.copy(out=b_all[:], in_=tiles["bias"][:, 0:H])
-
-        def do_rs(r):
+        def finish_one(r):
             i = r % 2
-            if ("res", r // 2) not in tiles:
-                tiles["res", r // 2] = tail.tile([P, 2 * H], F32, name="res")
-            res = tiles["res", r // 2]
-            nc.scalar.activation(res[:, H * i : H * i + H], tiles["sums", r // 2][:, H * i : H * i + H], ACT.Relu)
-            nc.sync.dma_start(out=o_view[r // 4][:, r % 4, :], in_=res[:, H * i : H * i + H])
+            if ("result", r // 2) not in held:
+                held["result", r // 2] = tail.tile([P, 2 * H], F32, name="result")
+            cols = slice(H * i, H * (i + 1))
+            result = held["result", r // 2]
+            nc.scalar.activation(result[:, cols], held["scaled", r // 2][:, cols], ACT.Relu)
+            nc.sync.dma_start(out=out_view[r // PACK][:, r % PACK, :], in_=result[:, cols])
 
-        table = {"wact": do_wact, "wcp": do_wcp, "wq": do_wq, "deg": do_deg, "pm": do_pm, "pow": do_pow, "tr": do_tr, "cp": do_cp, "q": do_q, "htr": do_htr, "hcp": do_hcp, "hq": do_hq, "xw": do_xw, "yt": do_yt, "yq": do_yq, "ys": do_ys, "yi": do_yi, "gg": do_gg, "dega": do_dega, "biasm": do_biasm, "biasc": do_biasc, "rs": do_rs, "aga": do_aga, "ag": do_ag, "st": do_st, "rl": do_rl}
-        for token in ORDER:
-            word = token.replace(".", " ")
-            names = [n for n in table if word.startswith(n) and all(ch in "0123456789 " for ch in word[len(n) :])]
-            n = names[0]
-            table[n](*[int(v) for v in word[len(n) :].split(" ") if v])
+        steps = {
+            "degree_half": degree_half, "degree": degree_of, "partial": partial, "root": inverse_root,
+            "turn": turn, "copy": copy_turned, "quantise": quantise,
+            "h_turn": h_turn, "h_copy": h_copy, "h_quantise": h_quantise,
+            "w_widen": w_widen, "w_group": w_group, "w_quantise": w_quantise,
+            "project": project, "scale_y": scale_y, "y_quantise": y_quantise,
+            "bias_spread": bias_spread, "bias_copy": bias_copy,
+            "aggregate": aggregate, "aggregate_last": aggregate_last,
+            "scale_sum": scale_sum, "finish_pair": finish_pair, "finish_one": finish_one,
+        }
+        for step in ORDER.split():
+            parts = step.split(":")
+            steps[parts[0]](*[int(part) for part in parts[1:]])

from contextlib import ExitStack

import concourse.mybir as mybir
from concourse.masks import make_identity

N, E, H = 2048, 512, 256
FLOPS = 2 * N * E * H + 2 * N * N * H

F32 = mybir.dt.float32
BF16 = mybir.dt.bfloat16
U32 = mybir.dt.uint32
U8 = mybir.dt.uint8
FP8 = mybir.dt.float8_e4m3fn
FP8X4 = mybir.dt.float8_e4m3fn_x4
ALU = mybir.AluOpType
ACT = mybir.ActivationFunctionType

P = 128
PACK = 4
PASS = P * PACK
GROUPS = N // PASS
TILES = N // P

DEGREE = "VVVVVTVVVSVVVTTV"

LOADS = """
half:0 half:1 w:0 adj:1 adj:2 bias:0 adj:3 adj:4 adj:5 adj:6 h:0 h:1 adj:7 h:2 adj:8 adj:9 h:3 adj:10 adj:11 adj:12
adj:13 adj:14 adj:15
"""

ORDER = """
degree_half:0 w_widen degree_half:1 turn:0:0 turn:0:1 degree:1 copy:0:0 w_group degree:2 turn:1:0 turn:1:1 copy:0:1
degree:3 turn:2:0 copy:1:0 turn:2:1 copy:1:1 quantise:0 turn:3:0 root:0 w_quantise copy:2:0 turn:3:1 degree:4
partial:5 copy:2:1 copy:3:0 degree:6 copy:3:1 turn:4:0 turn:4:1 degree:5 copy:4:0 h_turn:0:0 quantise:1 copy:4:1
h_turn:0:1 quantise:2 h_copy:0:0 h_turn:1:0 quantise:3 h_copy:0:1 h_turn:1:1 quantise:4 h_copy:1:0 turn:5:0 degree:7
turn:5:1 h_copy:1:1 h_turn:2:0 copy:5:0 h_quantise:0 h_turn:2:1 copy:5:1 h_quantise:1 turn:6:0 h_copy:2:0 turn:6:1
degree:8 h_copy:2:1 turn:7:0 turn:7:1 root:1 copy:6:0 project:0:0 h_quantise:2 copy:6:1 project:0:1 quantise:5
project:1:0 copy:7:0 project:1:1 scale_y:0:0 project:2:0 copy:7:1 scale_y:0:1 project:2:1 degree:9 bias_spread
scale_y:1:0 h_turn:3:0 y_quantise:0 h_turn:3:1 scale_y:1:1 turn:8:0 degree:10 turn:8:1 bias_copy turn:9:0 h_copy:3:0
turn:9:1 y_quantise:1 h_copy:3:1 degree:11 partial:13 copy:8:0 copy:8:1 h_quantise:3 partial:14 root:2 copy:9:0
degree:12 copy:9:1 degree:13 turn:10:0 scale_y:2:0 degree:14 turn:10:1 scale_y:2:1 copy:10:0 turn:11:0 turn:11:1
degree:15 copy:10:1 turn:12:0 copy:11:0 turn:12:1 y_quantise:2 copy:11:1 turn:13:0 quantise:6 turn:13:1 root:3
copy:12:0 quantise:7 turn:14:0 copy:12:1 quantise:8 turn:14:1 copy:13:0 quantise:9 turn:15:0 copy:13:1 turn:15:1
quantise:10 project:3:0 copy:14:0 quantise:11 project:3:1 copy:14:1 scale_y:3:0 aggregate:0 copy:15:0 aggregate:1
scale_y:3:1 copy:15:1 aggregate:2 quantise:12 aggregate:3 y_quantise:3 aggregate:4 quantise:13 aggregate:5 quantise:14
aggregate_last:0 aggregate_last:1 aggregate_last:2 aggregate_last:3 scale_sum:0 aggregate_last:4 aggregate_last:5
scale_sum:1 aggregate:6 scale_sum:2 aggregate:7 finish_pair:1 scale_sum:3 aggregate_last:6 scale_sum:4 aggregate:8
finish_pair:3 scale_sum:5 aggregate_last:7 scale_sum:6 aggregate:9 finish_pair:5 scale_sum:7 aggregate_last:8
aggregate:10 quantise:15 finish_pair:7 aggregate_last:9 aggregate:11 scale_sum:8 scale_sum:9 aggregate_last:10
aggregate:12 scale_sum:10 finish_pair:9 aggregate_last:11 aggregate:13 scale_sum:11 aggregate_last:12 aggregate:14
scale_sum:12 finish_pair:11 aggregate_last:13 aggregate:15 scale_sum:13 aggregate_last:14 aggregate_last:15
scale_sum:14 finish_pair:13 scale_sum:15 finish_one:14 finish_one:15
"""


def tile_gcnclassifer_pa_kernel(tc, h_enc, adj, w_bytes, w_scale, bias, out):
    nc = tc.nc
    h_view = h_enc.rearrange("(g p s) e -> g p s e", p=P, s=PACK)
    adj_view = adj.rearrange("(g p s) j -> g s p j", p=P, s=PACK)
    out_view = out.rearrange("(g p s) n -> g p s n", p=P, s=PACK)

    with ExitStack() as ctx:
        keep = ctx.enter_context(tc.tile_pool(name="keep", bufs=1))
        work = ctx.enter_context(tc.tile_pool(name="work", bufs=2))
        reordered = ctx.enter_context(tc.tile_pool(name="reordered", bufs=8))
        tail = ctx.enter_context(tc.tile_pool(name="tail", bufs=4))
        banks = ctx.enter_context(tc.psum_pool(name="banks", bufs=8))
        ctx.enter_context(tc.manual_schedule())

        adj_raw = [keep.tile([P, N], BF16, name=f"adj_raw{r}", align_bytes=64) for r in range(TILES)]
        adj_codes = [keep.tile([P, PASS], U32, name=f"adj_codes{r}", align_bytes=64) for r in range(TILES)]
        adj_scales = [keep.tile([P, PASS], U8, name=f"adj_scales{r}", align_bytes=64) for r in range(TILES)]
        h_raw = [keep.tile([P, PACK * E], BF16, name=f"h_raw{g}", align_bytes=64) for g in range(GROUPS)]
        h_codes = [keep.tile([P, PASS], U32, name=f"h_codes{g}", align_bytes=64) for g in range(GROUPS)]
        h_scales = [keep.tile([P, PASS], U8, name=f"h_scales{g}", align_bytes=64) for g in range(GROUPS)]
        y_codes = [keep.tile([P, H], U32, name=f"y_codes{g}", align_bytes=64) for g in range(GROUPS)]
        y_scales = [keep.tile([P, H], U8, name=f"y_scales{g}", align_bytes=64) for g in range(GROUPS)]
        w_raw = keep.tile([P, PACK * H], U8, name="w_raw", align_bytes=64)
        w_factor = keep.tile([P, PACK], F32, name="w_factor")
        w_wide = keep.tile([P, PACK, H], BF16, name="w_wide", align_bytes=64)
        w_grouped = keep.tile([P, H, PACK], BF16, name="w_grouped", align_bytes=64)
        w_codes = keep.tile([P, H], U32, name="w_codes", align_bytes=64)
        w_scales = keep.tile([P, H], U8, name="w_scales", align_bytes=64)
        identity = keep.tile([P, P], F32, name="identity")
        identity_bf16 = keep.tile([P, P], BF16, name="identity_bf16")
        ones = keep.tile([P, P], BF16, name="ones")
        bias_row = keep.tile([P, H], BF16, name="bias_row")
        bias_all = keep.tile([P, H], F32, name="bias_all")
        degree = keep.tile([P, TILES], F32, name="degree")
        dis = keep.tile([P, TILES], F32, name="dis")
        half_degree = keep.tile([P, 1], F32, name="half_degree")
        unused = keep.tile([P, P], F32, name="unused")
        table_load = keep.tile([P, 1], F32, name="table_load")

        nc.vector.memset(bias_row[:], 0.0)
        for load in LOADS.split():
            name, index = load.split(":")
            if name == "w":
                nc.sync.dma_start(out=w_raw[:].rearrange("p (t n) -> p t n", t=PACK), in_=w_bytes.rearrange("(p t) n -> p t n", t=PACK))
                nc.sync.dma_start(out=w_factor[:], in_=w_scale.rearrange("(p t) o -> p (t o)", t=PACK))
            elif name == "bias":
                nc.sync.dma_start(out=bias_row[0:1, :], in_=bias.rearrange("(o n) -> o n", o=1))
            elif name == "half":
                cols = slice(N // 2 * int(index), N // 2 * (int(index) + 1))
                nc.sync.dma_start(out=adj_raw[0][:, cols], in_=adj_view[0, 0][:, cols])
            elif name == "adj":
                nc.sync.dma_start(out=adj_raw[int(index)][:], in_=adj_view[int(index) // PACK, int(index) % PACK])
            else:
                nc.sync.dma_start(out=h_raw[int(index)][:].rearrange("p (s e) -> p s e", s=PACK), in_=h_view[int(index)])

        nc.vector.memset(table_load[:], 1.0)
        make_identity(nc, identity[:])
        nc.vector.memset(ones[:], 1.0)
        make_identity(nc, identity_bf16[:])
        nc.scalar.activation(table_load[:], table_load[:], ACT.Abs_reciprocal_sqrt)

        held = {}

        def word_order(tile, low, high):
            return tile[:, PACK * low : PACK * high].rearrange("p (n u e) -> p u n e", u=2, e=2)

        def by_u(tile, low, high):
            return tile[:].rearrange("p (u n e) -> p u n e", u=2, e=2)[:, :, low:high, :]

        def degree_half(half):
            if half == 0:
                held["reordered", 0] = reordered.tile([P, N], BF16, name="adj_reordered", align_bytes=64)
            low, high = N // 8 * half, N // 8 * (half + 1)
            nc.vector.tensor_scalar(
                out=by_u(held["reordered", 0], low, high),
                in0=word_order(adj_raw[0], low, high),
                scalar1=1.0,
                scalar2=half_degree[:] if half else None,
                op0=ALU.mult,
                op1=ALU.add,
                accum_out=degree[:, 0:1] if half else half_degree[:],
            )

        def degree_of(r):
            col = degree[:, r : r + 1]
            if DEGREE[r] == "T":
                nc.scalar.activation(unused[:], held["partial", r][:, 0:P], ACT.Copy, accum_out=col)
                return
            held["reordered", r] = reordered.tile([P, N], BF16, name="adj_reordered", align_bytes=64)
            src = word_order(adj_raw[r], 0, N // PACK)
            dst = by_u(held["reordered", r], 0, N // PACK)
            if DEGREE[r] == "S":
                nc.scalar.activation(dst, src, ACT.Copy, accum_out=col)
            else:
                nc.vector.tensor_scalar(out=dst, in0=src, scalar1=1.0, scalar2=None, op0=ALU.mult, op1=ALU.add, accum_out=col)

        def partial(r):
            bank = banks.tile([P, PASS], F32, name="bank")
            held["partial", r] = bank
            blocks = N // P
            for b in range(blocks):
                nc.tensor.matmul(bank[:, 0:P], lhsT=identity_bf16[:], rhs=adj_raw[r][:, P * b : P * b + P], start=(b == 0), stop=(b == blocks - 1))

        def inverse_root(g):
            cols = slice(PACK * g, PACK * g + PACK)
            nc.scalar.activation(dis[:, cols], degree[:, cols], ACT.Abs_reciprocal_sqrt)

        def turn(r, half):
            bank = banks.tile([P, PASS], F32, name="bank")
            held["turned", r, half] = bank
            for i in range(2):
                c = 2 * half + i
                for u in range(2):
                    if DEGREE[r] == "T":
                        words = adj_raw[r][:].bitcast(F32)[:, 2 * P * c + u : 2 * P * (c + 1) : 2]
                    else:
                        words = held["reordered", r][:].bitcast(F32)[:, N // 4 * u + P * c : N // 4 * u + P * (c + 1)]
                    nc.tensor.transpose(bank[:, P * (2 * i + u) : P * (2 * i + u + 1)], words, identity[:])

        def copy_turned(r, half):
            if ("grouped", r) not in held:
                held["grouped", r] = work.tile([P, N], BF16, name="adj_grouped", align_bytes=64) if DEGREE[r] == "T" else adj_raw[r]
            nc.scalar.copy(
                out=held["grouped", r][:].bitcast(F32)[:, PASS * half : PASS * (half + 1)].rearrange("p (c i u) -> p c i u", c=2, u=2),
                in_=held["turned", r, half][:].rearrange("p (c u i) -> p c i u", c=2, u=2),
            )

        def quantise(r):
            nc.vector.quantize_mx(out=adj_codes[r][:].bitcast(FP8X4), scales=adj_scales[r][:], in_=held["grouped", r][:])

        def h_turn(g, half):
            bank = banks.tile([P, PASS], F32, name="bank")
            held["h_turned", g, half] = bank
            words = h_raw[g][:].bitcast(F32)
            for i in range(2):
                s = 2 * half + i
                for u in range(2):
                    nc.tensor.transpose(bank[:, P * (2 * i + u) : P * (2 * i + u + 1)], words[:, 2 * P * s + u : 2 * P * (s + 1) : 2], identity[:])

        def h_copy(g, half):
            if ("h_grouped", g) not in held:
                held["h_grouped", g] = work.tile([P, PACK * E], BF16, name="h_grouped", align_bytes=64)
            nc.scalar.copy(
                out=held["h_grouped", g][:].bitcast(F32)[:, PASS * half : PASS * (half + 1)].rearrange("p (s i u) -> p s i u", s=2, u=2),
                in_=held["h_turned", g, half][:].rearrange("p (s u i) -> p s i u", s=2, u=2),
            )

        def h_quantise(g):
            nc.vector.quantize_mx(out=h_codes[g][:].bitcast(FP8X4), scales=h_scales[g][:], in_=held["h_grouped", g][:])

        def w_widen():
            for t in range(PACK):
                nc.scalar.activation(w_wide[:, t, :], w_raw[:, H * t : H * (t + 1)].bitcast(FP8), ACT.Copy, scale=w_factor[:, t : t + 1])

        def w_group():
            nc.scalar.copy(out=w_grouped[:], in_=w_wide[:].rearrange("p t n -> p n t"))

        def w_quantise():
            nc.vector.quantize_mx(out=w_codes[:].bitcast(FP8X4), scales=w_scales[:], in_=w_grouped[:].rearrange("p n t -> p (n t)"))

        def project(g, half):
            cols = slice(P * half, P * (half + 1))
            bank = banks.tile([P, PASS], F32, name="bank")
            held["xw", g, half] = bank
            for s in range(PACK):
                rows = slice(P * s, P * (s + 1))
                nc.tensor.matmul_mx(
                    out=bank[:, rows],
                    lhsT=h_codes[g][:, rows].bitcast(FP8X4),
                    lhsT_scale=h_scales[g][:, rows],
                    rhs=w_codes[:, cols].bitcast(FP8X4),
                    rhs_scale=w_scales[:, cols],
                    start=True,
                    stop=True,
                )

        def scale_y(g, half):
            if ("y", g) not in held:
                held["y", g] = work.tile([P, PACK * H], BF16, name="y_grouped", align_bytes=64)
            nc.vector.tensor_tensor(
                out=held["y", g][:, PASS * half : PASS * (half + 1)].rearrange("p (n s) -> p n s", s=PACK),
                in0=held["xw", g, half][:].rearrange("p (s n) -> p n s", s=PACK),
                in1=dis[:, PACK * g : PACK * (g + 1)].unsqueeze(1).to_broadcast([P, P, PACK]),
                op=ALU.mult,
            )

        def y_quantise(g):
            nc.vector.quantize_mx(out=y_codes[g][:].bitcast(FP8X4), scales=y_scales[g][:], in_=held["y", g][:])

        def aggregate_pass(r, c):
            rows = slice(P * c, P * (c + 1))
            nc.tensor.matmul_mx(
                out=held["sum", r][:, 0:H],
                lhsT=adj_codes[r][:, rows].bitcast(FP8X4),
                lhsT_scale=adj_scales[r][:, rows],
                rhs=y_codes[c][:].bitcast(FP8X4),
                rhs_scale=y_scales[c][:],
                start=(c == 0),
                stop=(c == GROUPS - 1),
            )

        def aggregate(r):
            held["sum", r] = banks.tile([P, PASS], F32, name="bank")
            for c in range(GROUPS - 1):
                aggregate_pass(r, c)

        def aggregate_last(r):
            aggregate_pass(r, GROUPS - 1)

        def bias_spread():
            held["bias", 0] = banks.tile([P, PASS], F32, name="bank")
            nc.tensor.matmul(held["bias", 0][:, 0:H], lhsT=ones[:], rhs=bias_row[:], start=True, stop=True)

        def bias_copy():
            nc.scalar.copy(out=bias_all[:], in_=held["bias", 0][:, 0:H])

        def scale_sum(r):
            i = r % 2
            if ("scaled", r // 2) not in held:
                held["scaled", r // 2] = tail.tile([P, 2 * H], F32, name="scaled")
            nc.vector.scalar_tensor_tensor(
                out=held["scaled", r // 2][:, H * i : H * (i + 1)],
                in0=held["sum", r][:, 0:H],
                scalar=dis[:, r : r + 1],
                in1=bias_all[:],
                op0=ALU.mult,
                op1=ALU.add,
            )

        def finish_pair(r):
            pair = r // 2
            result = tail.tile([P, 2 * H], F32, name="result")
            nc.scalar.activation(result[:], held["scaled", pair][:], ACT.Relu)
            s = 2 * (pair % 2)
            nc.sync.dma_start(out=out_view[pair // 2][:, s : s + 2, :], in_=result[:].rearrange("p (s n) -> p s n", s=2))

        def finish_one(r):
            i = r % 2
            if ("result", r // 2) not in held:
                held["result", r // 2] = tail.tile([P, 2 * H], F32, name="result")
            cols = slice(H * i, H * (i + 1))
            result = held["result", r // 2]
            nc.scalar.activation(result[:, cols], held["scaled", r // 2][:, cols], ACT.Relu)
            nc.sync.dma_start(out=out_view[r // PACK][:, r % PACK, :], in_=result[:, cols])

        steps = {
            "degree_half": degree_half, "degree": degree_of, "partial": partial, "root": inverse_root,
            "turn": turn, "copy": copy_turned, "quantise": quantise,
            "h_turn": h_turn, "h_copy": h_copy, "h_quantise": h_quantise,
            "w_widen": w_widen, "w_group": w_group, "w_quantise": w_quantise,
            "project": project, "scale_y": scale_y, "y_quantise": y_quantise,
            "bias_spread": bias_spread, "bias_copy": bias_copy,
            "aggregate": aggregate, "aggregate_last": aggregate_last,
            "scale_sum": scale_sum, "finish_pair": finish_pair, "finish_one": finish_one,
        }
        for step in ORDER.split():
            parts = step.split(":")
            steps[parts[0]](*[int(part) for part in parts[1:]])
